import numpy as np
import ml_dtypes


def mxq(x, axis, fmt="e4m3"):
    dtype, down = {"e4m3": (ml_dtypes.float8_e4m3fn, 7), "e5m2": (ml_dtypes.float8_e5m2, 14)}[fmt]
    v = np.moveaxis(np.asarray(x, np.float32).astype(ml_dtypes.bfloat16).astype(np.float64), axis, -1)
    blocks = v.reshape(v.shape[:-1] + (-1, 32))
    amax = np.abs(blocks).max(-1, keepdims=True)
    byte = np.maximum(np.where(amax > 0, np.frexp(amax)[1] - 1 + 127, 0) - down, 1)
    scale = np.exp2(byte - 127.0)
    codes = (blocks / scale).astype(np.float32).astype(dtype).astype(np.float64)
    return np.moveaxis((codes * scale).reshape(v.shape), -1, axis)


WIDE = False


def mx_kscale(k):
    if not WIDE:
        return np.ones(k)
    levels = np.array([10, -10, 5, -5, 0])
    a = np.random.permutation(np.resize(levels, k // 512 * 4)).reshape(k // 512, 4)
    idx = np.arange(k)
    return np.exp2(a[idx // 512, idx % 128 // 32])


BF16 = ml_dtypes.bfloat16


def bf(x):
    return np.asarray(x, np.float32).astype(BF16)


def f64(x):
    return np.asarray(x).astype(np.float64)


B, N, D, F, M1, M2 = 4, 128, 512, 2048, 3, 5
EPS = 1e-12


def erf(z):
    a = np.clip(z, -6.0, 6.0)
    a2 = 2.0 * a * a
    term = a.copy()
    tot = a.copy()
    for k in range(1, 120):
        term = term * (a2 / (2 * k + 1))
        tot = tot + term
    return 2.0 / np.sqrt(np.pi) * np.exp(-a * a) * tot


def gelu(v):
    return 0.5 * v * (1.0 + erf(v / np.sqrt(2.0)))


def setup_inputs():
    s = mx_kscale(D)
    return {'x': bf(np.random.standard_normal((B, N, D, M2)) * s[:, None]),
            'w_in': bf(np.random.standard_normal((D, F)) / np.sqrt(D) / s[:, None]),
            'scale': bf(1.0 + 0.1 * np.random.standard_normal((1, 1, F))),
            'bias': bf(0.3 * np.random.standard_normal((1, 1, F))),
            'w_out': bf(np.random.standard_normal((F, D)) / np.sqrt(F))}


def reference(x, w_in, scale, bias, w_out):
    xq = mxq(f64(x), 2, 'e4m3')
    h = np.swapaxes(np.swapaxes(xq, -1, -2) @ mxq(f64(w_in), 0, 'e4m3'), -1, -2)
    norm = np.maximum(np.sqrt(np.sum(h * h, axis=-1, keepdims=True)), EPS)
    phase = h / norm
    gated = gelu(norm[..., 0] * f64(scale) + f64(bias))[..., None]
    g = gated * phase
    y = np.swapaxes(mxq(g, 2, 'e4m3'), -1, -2) @ mxq(f64(w_out), 0, 'e4m3')
    return np.swapaxes(y, -1, -2)

@@ -1,0 +1,238 @@
+from contextlib import ExitStack
+
+import concourse.mybir as mybir
+from concourse.masks import make_identity
+
+F32 = mybir.dt.float32
+BF16 = mybir.dt.bfloat16
+U32 = mybir.dt.uint32
+U8 = mybir.dt.uint8
+FP8X4 = mybir.dt.float8_e4m3fn_x4
+ACT = mybir.ActivationFunctionType
+ALU = mybir.AluOpType
+
+P = 128
+PACK = 4
+K_PASS = P * PACK
+TOKEN_TILES = 4
+D = 512
+F = 2048
+F_GROUPS = F // K_PASS
+M2 = 5
+EPS = 1e-12
+
+FLOPS = 2 * 2 * (TOKEN_TILES * P * M2) * D * F
+
+
+def tile_feedforwardse3_pb_kernel(tc, x, w_in, scale, bias, w_out, out):
+    nc = tc.nc
+    with ExitStack() as stack:
+        consts = stack.enter_context(tc.tile_pool(name="consts", bufs=1))
+        keep = stack.enter_context(tc.tile_pool(name="keep", bufs=1))
+        x_stage = stack.enter_context(tc.tile_pool(name="x_stage", bufs=2))
+        w_stage = stack.enter_context(tc.tile_pool(name="w_stage", bufs=3))
+        work = stack.enter_context(tc.tile_pool(name="work", bufs=2))
+        per_tile = stack.enter_context(tc.tile_pool(name="per_tile", bufs=2))
+        chain = stack.enter_context(tc.tile_pool(name="chain", bufs=1))
+        psum_x = stack.enter_context(tc.psum_pool(name="psum_x", bufs=1))
+        psum_norm = stack.enter_context(tc.psum_pool(name="psum_norm", bufs=2))
+        psum_gate = stack.enter_context(tc.psum_pool(name="psum_gate", bufs=3))
+        psum_out = stack.enter_context(tc.psum_pool(name="psum_out", bufs=2))
+
+        identity = consts.tile([P, P], F32)
+        make_identity(nc, identity[:])
+
+        x_codes = keep.tile([P, TOKEN_TILES, M2, P], U32, align_bytes=64)
+        x_scales = keep.tile([P, TOKEN_TILES, M2, P], U8, align_bytes=64)
+        w1_codes = keep.tile([P, F_GROUPS, K_PASS], U32, align_bytes=64)
+        w1_scales = keep.tile([P, F_GROUPS, K_PASS], U8, align_bytes=64)
+        w2_codes = keep.tile([P, F_GROUPS, D], U32, align_bytes=64)
+        w2_scales = keep.tile([P, F_GROUPS, D], U8, align_bytes=64)
+
+        def quantise_x(tt):
+            x_rows = x_stage.tile([P, D * M2], BF16)
+            nc.sync.dma_start(out=x_rows[:], in_=x[tt].rearrange("n d m -> n (d m)"))
+            x_sorted = x_stage.tile([P, M2 * D], BF16)
+            nc.vector.tensor_copy(
+                out=x_sorted[:].rearrange("t (m u p e) -> t m u p e", m=M2, u=2, p=P, e=2),
+                in_=x_rows[:].rearrange("t (p u e m) -> t m u p e", p=P, u=2, e=2, m=M2),
+            )
+            x_pairs = x_sorted[:].bitcast(F32)
+            x_grouped = x_stage.tile([P, M2, K_PASS], BF16, align_bytes=64)
+            for m in range(M2):
+                x_t = psum_x.tile([P, 2, P], F32)
+                for u in range(2):
+                    first = (2 * m + u) * P
+                    nc.tensor.transpose(x_t[:, u, :], x_pairs[:, first : first + P], identity[:])
+                nc.scalar.copy(
+                    out=x_grouped[:, m, :].bitcast(F32).rearrange("p (t u) -> p t u", u=2),
+                    in_=x_t[:].rearrange("p u t -> p t u"),
+                )
+            for m in range(M2):
+                nc.vector.quantize_mx(
+                    out=x_codes[:, tt, m, :].bitcast(FP8X4),
+                    scales=x_scales[:, tt, m, :],
+                    in_=x_grouped[:, m, :],
+                )
+
+        def quantise_w_in(fg):
+            w_rows = w_stage.tile([P, PACK, K_PASS], BF16, tag="w_rows")
+            f_cols = slice(fg * K_PASS, (fg + 1) * K_PASS)
+            nc.sync.dma_start(
+                out=w_rows[:], in_=w_in[:, f_cols].rearrange("(q s) f -> q s f", s=PACK)
+            )
+            w_grouped = w_stage.tile([P, K_PASS * PACK], BF16, tag="w_grouped", align_bytes=64)
+            nc.vector.tensor_copy(
+                out=w_grouped[:].rearrange("q (j p s) -> q j p s", j=PACK, p=P, s=PACK),
+                in_=w_rows[:].rearrange("q s (p j) -> q j p s", j=PACK),
+            )
+            nc.vector.quantize_mx(
+                out=w1_codes[:, fg, :].bitcast(FP8X4), scales=w1_scales[:, fg, :], in_=w_grouped[:]
+            )
+
+        def quantise_w_out(fg):
+            w_rows = w_stage.tile([P, PACK, D], BF16, tag="w_rows")
+            f_rows = slice(fg * K_PASS, (fg + 1) * K_PASS)
+            nc.sync.dma_start(
+                out=w_rows[:], in_=w_out[f_rows, :].rearrange("(p j) d -> p j d", j=PACK)
+            )
+            w_grouped = w_stage.tile([P, D * PACK], BF16, tag="w_grouped", align_bytes=64)
+            nc.vector.tensor_copy(
+                out=w_grouped[:].rearrange("p (d j) -> p d j", j=PACK),
+                in_=w_rows[:].rearrange("p j d -> p d j"),
+            )
+            nc.vector.quantize_mx(
+                out=w2_codes[:, fg, :].bitcast(FP8X4), scales=w2_scales[:, fg, :], in_=w_grouped[:]
+            )
+
+        def first_matmul(h, tt, fg, m):
+            for j in range(PACK):
+                cols = slice(j * P, (j + 1) * P)
+                nc.tensor.matmul_mx(
+                    out=h[:, j, :],
+                    lhsT=w1_codes[:, fg, cols].bitcast(FP8X4),
+                    lhsT_scale=w1_scales[:, fg, cols],
+                    rhs=x_codes[:, tt, m, :].bitcast(FP8X4),
+                    rhs_scale=x_scales[:, tt, m, :],
+                    start=True,
+                    stop=True,
+                )
+
+        def norms_of_unit(tt, fg, inv_norm, norm):
+            squares = work.tile([P, M2, K_PASS], F32)
+            for m in range(M2):
+                h = psum_norm.tile([P, PACK, P], F32)
+                first_matmul(h, tt, fg, m)
+                nc.scalar.activation(
+                    out=squares[:, m, :], in_=h[:].rearrange("p j t -> p (j t)"), func=ACT.Square
+                )
+            pairs = work.tile([P, 2, K_PASS], F32)
+            nc.vector.tensor_add(out=pairs[:], in0=squares[:, 0:2, :], in1=squares[:, 2:4, :])
+            total = work.tile([P, K_PASS], F32)
+            nc.vector.tensor_add(out=total[:], in0=pairs[:, 0, :], in1=pairs[:, 1, :])
+            nc.vector.tensor_add(out=total[:], in0=total[:], in1=squares[:, 4, :])
+            nc.vector.tensor_scalar_max(out=total[:], in0=total[:], scalar1=EPS * EPS)
+            nc.scalar.activation(out=inv_norm[:, fg, :], in_=total[:], func=ACT.Abs_reciprocal_sqrt)
+            nc.vector.tensor_mul(out=norm[:, fg, :], in0=total[:], in1=inv_norm[:, fg, :])
+
+        def gate_of_tile(inv_norm, norm, gate):
+            for fg in range(F_GROUPS):
+                for j in range(PACK):
+                    cols = slice(j * P, (j + 1) * P)
+                    c = fg * PACK + j
+                    nc.scalar.activation(
+                        out=gate[:, fg, cols],
+                        in_=norm[:, fg, cols],
+                        func=ACT.Gelu,
+                        scale=gain[:, c : c + 1],
+                        bias=shift[:, c : c + 1],
+                    )
+                nc.vector.tensor_mul(out=gate[:, fg, :], in0=gate[:, fg, :], in1=inv_norm[:, fg, :])
+
+        def gated_unit(tt, fg, gate, g_codes, g_scales):
+            g_grouped = work.tile([P, M2, P, PACK], BF16, align_bytes=64)
+            for m in range(M2):
+                h = psum_gate.tile([P, PACK, P], F32)
+                first_matmul(h, tt, fg, m)
+                nc.vector.tensor_tensor(
+                    out=g_grouped[:, m, :, :],
+                    in0=h[:].rearrange("p j t -> p t j"),
+                    in1=gate[:, fg, :].rearrange("p (j t) -> p t j", j=PACK),
+                    op=ALU.mult,
+                )
+            for first, last in ((0, 4), (4, 5)):
+                nc.vector.quantize_mx(
+                    out=g_codes[:, fg, first:last, :].rearrange("p m t -> p (m t)").bitcast(FP8X4),
+                    scales=g_scales[:, fg, first:last, :].rearrange("p m t -> p (m t)"),
+                    in_=g_grouped[:, first:last, :, :].rearrange("p m t j -> p (m t j)"),
+                )
+
+        def second_matmul(tt, g_codes, g_scales):
+            y_planes = per_tile.tile([P, M2, D], F32, tag="y_planes")
+            for m in range(M2):
+                y = psum_out.tile([P, D], F32)
+                for fg in range(F_GROUPS):
+                    nc.tensor.matmul_mx(
+                        out=y[:],
+                        lhsT=g_codes[:, fg, m, :].bitcast(FP8X4),
+                        lhsT_scale=g_scales[:, fg, m, :],
+                        rhs=w2_codes[:, fg, :].bitcast(FP8X4),
+                        rhs_scale=w2_scales[:, fg, :],
+                        start=(fg == 0),
+                        stop=(fg == F_GROUPS - 1),
+                    )
+                nc.scalar.copy(out=y_planes[:, m, :], in_=y[:])
+            y_rows = per_tile.tile([P, D, M2], F32, tag="y_rows")
+            nc.gpsimd.tensor_scalar(
+                out=y_rows[:],
+                in0=y_planes[:].rearrange("t m d -> t d m"),
+                scalar1=1.0,
+                scalar2=0.0,
+                op0=ALU.mult,
+                op1=ALU.add,
+            )
+            nc.sync.dma_start(
+                out=out[tt].rearrange("n d m -> n (d m)"), in_=y_rows[:].rearrange("t d m -> t (d m)")
+            )
+
+        def new_norm_tiles():
+            inv_norm = chain.tile([P, F_GROUPS, K_PASS], F32, tag="inv_norm")
+            norm = chain.tile([P, F_GROUPS, K_PASS], F32, tag="norm")
+            return inv_norm, norm
+
+        gain_bf = consts.tile([P, F_GROUPS, PACK], BF16)
+        shift_bf = consts.tile([P, F_GROUPS, PACK], BF16)
+        by_partition = "a b (g p j) -> p (a b g) j"
+        nc.scalar.dma_start(out=gain_bf[:], in_=scale.rearrange(by_partition, p=P, j=PACK))
+        nc.scalar.dma_start(out=shift_bf[:], in_=bias.rearrange(by_partition, p=P, j=PACK))
+        gain = consts.tile([P, F_GROUPS * PACK], F32)
+        shift = consts.tile([P, F_GROUPS * PACK], F32)
+        nc.vector.tensor_copy(out=gain[:], in_=gain_bf[:].rearrange("p g j -> p (g j)"))
+        nc.vector.tensor_copy(out=shift[:], in_=shift_bf[:].rearrange("p g j -> p (g j)"))
+
+        quantise_x(0)
+        for fg in range(F_GROUPS):
+            quantise_w_in(fg)
+        inv_norm, norm = new_norm_tiles()
+        for fg in range(F_GROUPS):
+            norms_of_unit(0, fg, inv_norm, norm)
+        for fg in range(F_GROUPS):
+            quantise_w_out(fg)
+        gate = per_tile.tile([P, F_GROUPS, K_PASS], F32, tag="gate")
+        gate_of_tile(inv_norm, norm, gate)
+
+        for tt in range(TOKEN_TILES):
+            ahead = tt + 1 < TOKEN_TILES
+            g_codes = per_tile.tile([P, F_GROUPS, M2, P], U32, tag="g_codes", align_bytes=64)
+            g_scales = per_tile.tile([P, F_GROUPS, M2, P], U8, tag="g_scales", align_bytes=64)
+            if ahead:
+                quantise_x(tt + 1)
+                inv_norm, norm = new_norm_tiles()
+            for fg in range(F_GROUPS):
+                if ahead:
+                    norms_of_unit(tt + 1, fg, inv_norm, norm)
+                gated_unit(tt, fg, gate, g_codes, g_scales)
+            if ahead:
+                gate = per_tile.tile([P, F_GROUPS, K_PASS], F32, tag="gate")
+                gate_of_tile(inv_norm, norm, gate)
+            second_matmul(tt, g_codes, g_scales)

@@ -18,8 +18,11 @@ TOKEN_TILES = 4
 D = 512
 F = 2048
 F_GROUPS = F // K_PASS
+UNITS = TOKEN_TILES * F_GROUPS
 M2 = 5
 EPS = 1e-12
+
+LEAD = 6
 
 FLOPS = 2 * 2 * (TOKEN_TILES * P * M2) * D * F
 
@@ -29,15 +32,17 @@ def tile_feedforwardse3_pb_kernel(tc, x, w_in, scale, bias, w_out, out):
     with ExitStack() as stack:
         consts = stack.enter_context(tc.tile_pool(name="consts", bufs=1))
         keep = stack.enter_context(tc.tile_pool(name="keep", bufs=1))
-        x_stage = stack.enter_context(tc.tile_pool(name="x_stage", bufs=2))
-        w_stage = stack.enter_context(tc.tile_pool(name="w_stage", bufs=3))
-        work = stack.enter_context(tc.tile_pool(name="work", bufs=2))
-        per_tile = stack.enter_context(tc.tile_pool(name="per_tile", bufs=2))
-        chain = stack.enter_context(tc.tile_pool(name="chain", bufs=1))
-        psum_x = stack.enter_context(tc.psum_pool(name="psum_x", bufs=1))
-        psum_norm = stack.enter_context(tc.psum_pool(name="psum_norm", bufs=2))
-        psum_gate = stack.enter_context(tc.psum_pool(name="psum_gate", bufs=3))
+        x_rows_pool = stack.enter_context(tc.tile_pool(name="x_rows_pool", bufs=2))
+        x_work = stack.enter_context(tc.tile_pool(name="x_work", bufs=1))
+        w_rows_pool = stack.enter_context(tc.tile_pool(name="w_rows_pool", bufs=4))
+        pairs_of = stack.enter_context(tc.tile_pool(name="pairs_of", bufs=2))
+        six_of = stack.enter_context(tc.tile_pool(name="six_of", bufs=6))
+        y_pool = stack.enter_context(tc.tile_pool(name="y_pool", bufs=1))
+        psum_norm = stack.enter_context(tc.psum_pool(name="psum_norm", bufs=3))
+        psum_sum = stack.enter_context(tc.psum_pool(name="psum_sum", bufs=1))
+        psum_gate = stack.enter_context(tc.psum_pool(name="psum_gate", bufs=2))
         psum_out = stack.enter_context(tc.psum_pool(name="psum_out", bufs=2))
+        stack.enter_context(tc.manual_schedule())
 
         identity = consts.tile([P, P], F32)
         make_identity(nc, identity[:])
@@ -49,24 +54,57 @@ def tile_feedforwardse3_pb_kernel(tc, x, w_in, scale, bias, w_out, out):
         w2_codes = keep.tile([P, F_GROUPS, D], U32, align_bytes=64)
         w2_scales = keep.tile([P, F_GROUPS, D], U8, align_bytes=64)
 
-        def quantise_x(tt):
-            x_rows = x_stage.tile([P, D * M2], BF16)
+        def load_x(tt):
+            x_rows = x_rows_pool.tile([P, D * M2], BF16, name="x_rows")
             nc.sync.dma_start(out=x_rows[:], in_=x[tt].rearrange("n d m -> n (d m)"))
-            x_sorted = x_stage.tile([P, M2 * D], BF16)
+            return x_rows
+
+        def load_weight_rows(weight, fg, by_columns):
+            w_rows = w_rows_pool.tile([P, PACK, K_PASS], BF16, name="w_rows")
+            piece = slice(fg * K_PASS, (fg + 1) * K_PASS)
+            source = weight[:, piece] if by_columns else weight[piece, :]
+            nc.sync.dma_start(out=w_rows[:], in_=source.rearrange("(q s) c -> q s c", s=PACK))
+            return w_rows
+
+        x_rows_of = [load_x(0)]
+        w_in_rows = [load_weight_rows(w_in, fg, True) for fg in range(F_GROUPS)]
+        x_rows_of.append(load_x(1))
+        w_out_rows = [load_weight_rows(w_out, fg, False) for fg in range(F_GROUPS)]
+        x_rows_of.extend([load_x(2), load_x(3)])
+
+        gain_bf = consts.tile([P, F_GROUPS, PACK], BF16)
+        shift_bf = consts.tile([P, F_GROUPS, PACK], BF16)
+        by_partition = "a b (g p j) -> p (a b g) j"
+        nc.scalar.dma_start(out=gain_bf[:], in_=scale.rearrange(by_partition, p=P, j=PACK))
+        nc.scalar.dma_start(out=shift_bf[:], in_=bias.rearrange(by_partition, p=P, j=PACK))
+        gain = consts.tile([P, F_GROUPS * PACK], F32)
+        shift = consts.tile([P, F_GROUPS * PACK], F32)
+
+        def sort_x(tt):
+            x_sorted = x_work.tile([P, M2 * D], BF16, name="x_sorted")
             nc.vector.tensor_copy(
                 out=x_sorted[:].rearrange("t (m u p e) -> t m u p e", m=M2, u=2, p=P, e=2),
-                in_=x_rows[:].rearrange("t (p u e m) -> t m u p e", p=P, u=2, e=2, m=M2),
+                in_=x_rows_of[tt][:].rearrange("t (p u e m) -> t m u p e", p=P, u=2, e=2, m=M2),
             )
+            return x_sorted
+
+        def pack_x(tt, x_sorted):
             x_pairs = x_sorted[:].bitcast(F32)
-            x_grouped = x_stage.tile([P, M2, K_PASS], BF16, align_bytes=64)
-            for m in range(M2):
-                x_t = psum_x.tile([P, 2, P], F32)
-                for u in range(2):
-                    first = (2 * m + u) * P
-                    nc.tensor.transpose(x_t[:, u, :], x_pairs[:, first : first + P], identity[:])
-                nc.scalar.copy(
-                    out=x_grouped[:, m, :].bitcast(F32).rearrange("p (t u) -> p t u", u=2),
-                    in_=x_t[:].rearrange("p u t -> p t u"),
+            x_grouped = x_work.tile([P, M2, K_PASS], BF16, name="x_grouped", align_bytes=64)
+            for first in range(0, M2, 2):
+                count = min(2, M2 - first)
+                x_t = psum_out.tile([P, 2, 2, P], F32, tag="bank")
+                for i in range(2 * count):
+                    start = (2 * first + i) * P
+                    nc.tensor.transpose(
+                        x_t[:, i // 2, i % 2, :], x_pairs[:, start : start + P], identity[:]
+                    )
+                nc.vector.tensor_copy(
+                    out=x_grouped[:, first : first + count, :]
+                    .rearrange("p m k -> p (m k)")
+                    .bitcast(F32)
+                    .rearrange("p (m t u) -> p m t u", m=count, u=2),
+                    in_=x_t[:, 0:count, :, :].rearrange("p m u t -> p m t u"),
                 )
             for m in range(M2):
                 nc.vector.quantize_mx(
@@ -76,36 +114,108 @@ def tile_feedforwardse3_pb_kernel(tc, x, w_in, scale, bias, w_out, out):
                 )
 
         def quantise_w_in(fg):
-            w_rows = w_stage.tile([P, PACK, K_PASS], BF16, tag="w_rows")
-            f_cols = slice(fg * K_PASS, (fg + 1) * K_PASS)
-            nc.sync.dma_start(
-                out=w_rows[:], in_=w_in[:, f_cols].rearrange("(q s) f -> q s f", s=PACK)
-            )
-            w_grouped = w_stage.tile([P, K_PASS * PACK], BF16, tag="w_grouped", align_bytes=64)
+            w_grouped = pairs_of.tile([P, K_PASS * PACK], BF16, name="w_grouped", align_bytes=64)
             nc.vector.tensor_copy(
                 out=w_grouped[:].rearrange("q (j p s) -> q j p s", j=PACK, p=P, s=PACK),
-                in_=w_rows[:].rearrange("q s (p j) -> q j p s", j=PACK),
+                in_=w_in_rows[fg][:].rearrange("q s (p j) -> q j p s", j=PACK),
             )
             nc.vector.quantize_mx(
                 out=w1_codes[:, fg, :].bitcast(FP8X4), scales=w1_scales[:, fg, :], in_=w_grouped[:]
             )
 
         def quantise_w_out(fg):
-            w_rows = w_stage.tile([P, PACK, D], BF16, tag="w_rows")
-            f_rows = slice(fg * K_PASS, (fg + 1) * K_PASS)
-            nc.sync.dma_start(
-                out=w_rows[:], in_=w_out[f_rows, :].rearrange("(p j) d -> p j d", j=PACK)
-            )
-            w_grouped = w_stage.tile([P, D * PACK], BF16, tag="w_grouped", align_bytes=64)
+            w_grouped = pairs_of.tile([P, D * PACK], BF16, name="w_grouped", align_bytes=64)
             nc.vector.tensor_copy(
                 out=w_grouped[:].rearrange("p (d j) -> p d j", j=PACK),
-                in_=w_rows[:].rearrange("p j d -> p d j"),
+                in_=w_out_rows[fg][:].rearrange("p j d -> p d j"),
             )
             nc.vector.quantize_mx(
                 out=w2_codes[:, fg, :].bitcast(FP8X4), scales=w2_scales[:, fg, :], in_=w_grouped[:]
             )
 
-        def first_matmul(h, tt, fg, m):
+        squares_of = {}
+        total_of = {}
+        inv_norm_of = {}
+        norm_of = {}
+        gate_of = {}
+        g_grouped_of = {}
+        g_words_of = {}
+        y_planes_of = {}
+
+        def square_component(unit, m):
+            tt, fg = divmod(unit, F_GROUPS)
+            if m == 0:
+                squares_of[unit] = pairs_of.tile([P, M2, K_PASS], F32, name="squares")
+            h_rows = psum_norm.tile([P, K_PASS], F32)
+            nc.tensor.matmul_mx(
+                out=h_rows[:],
+                lhsT=x_codes[:, tt, m, :].bitcast(FP8X4),
+                lhsT_scale=x_scales[:, tt, m, :],
+                rhs=w1_codes[:, fg, :].bitcast(FP8X4),
+                rhs_scale=w1_scales[:, fg, :],
+                start=True,
+                stop=True,
+            )
+            nc.scalar.activation(out=squares_of[unit][:, m, :], in_=h_rows[:], func=ACT.Square)
+
+        def sum_squares(unit):
+            sums = psum_sum.tile([P, PACK, P], F32)
+            for j in range(PACK):
+                for m in range(M2):
+                    nc.tensor.matmul(
+                        out=sums[:, j, :],
+                        lhsT=squares_of[unit][:, m, j * P : (j + 1) * P],
+                        rhs=identity[:],
+                        is_transpose=True,
+                        start=(m == 0),
+                        stop=(m == M2 - 1),
+                    )
+            return sums
+
+        def clamp_sums(unit, sums):
+            total_of[unit] = pairs_of.tile([P, K_PASS], F32, name="total")
+            nc.vector.tensor_scalar_max(
+                out=total_of[unit][:], in0=sums[:].rearrange("p j t -> p (j t)"), scalar1=EPS * EPS
+            )
+
+        def norm_of_unit(unit):
+            inv_norm_of[unit] = six_of.tile([P, K_PASS], F32, name="inv_norm")
+            norm_of[unit] = six_of.tile([P, K_PASS], F32, name="norm")
+            nc.scalar.activation(
+                out=inv_norm_of[unit][:], in_=total_of[unit][:], func=ACT.Abs_reciprocal_sqrt
+            )
+            nc.gpsimd.tensor_tensor(
+                out=norm_of[unit][:], in0=total_of[unit][:], in1=inv_norm_of[unit][:], op=ALU.mult
+            )
+
+        def gate_of_unit(unit):
+            fg = unit % F_GROUPS
+            gelu = norm_of[unit]
+            for j in range(PACK):
+                cols = slice(j * P, (j + 1) * P)
+                c = fg * PACK + j
+                nc.scalar.activation(
+                    out=gelu[:, cols],
+                    in_=gelu[:, cols],
+                    func=ACT.Gelu,
+                    scale=gain[:, c : c + 1],
+                    bias=shift[:, c : c + 1],
+                )
+            gate_of[unit] = six_of.tile([P, P, PACK], F32, name="gate")
+            nc.gpsimd.tensor_tensor(
+                out=gate_of[unit][:],
+                in0=gelu[:].rearrange("p (j t) -> p t j", j=PACK),
+                in1=inv_norm_of[unit][:].rearrange("p (j t) -> p t j", j=PACK),
+                op=ALU.mult,
+            )
+
+        def gate_component(unit, m):
+            tt, fg = divmod(unit, F_GROUPS)
+            if m == 0:
+                g_grouped_of[unit] = pairs_of.tile(
+                    [P, M2, P, PACK], BF16, name="g_grouped", align_bytes=64
+                )
+            h = psum_gate.tile([P, PACK, P], F32)
             for j in range(PACK):
                 cols = slice(j * P, (j + 1) * P)
                 nc.tensor.matmul_mx(
@@ -117,122 +227,111 @@ def tile_feedforwardse3_pb_kernel(tc, x, w_in, scale, bias, w_out, out):
                     start=True,
                     stop=True,
                 )
+            nc.vector.tensor_tensor(
+                out=g_grouped_of[unit][:, m, :, :],
+                in0=h[:].rearrange("p j t -> p t j"),
+                in1=gate_of[unit][:],
+                op=ALU.mult,
+            )
 
-        def norms_of_unit(tt, fg, inv_norm, norm):
-            squares = work.tile([P, M2, K_PASS], F32)
-            for m in range(M2):
-                h = psum_norm.tile([P, PACK, P], F32)
-                first_matmul(h, tt, fg, m)
-                nc.scalar.activation(
-                    out=squares[:, m, :], in_=h[:].rearrange("p j t -> p (j t)"), func=ACT.Square
+        def quantise_g(unit):
+            tt, fg = divmod(unit, F_GROUPS)
+            if fg == 0:
+                g_words_of[tt] = (
+                    pairs_of.tile([P, F_GROUPS, M2, P], U32, name="g_codes", align_bytes=64),
+                    pairs_of.tile([P, F_GROUPS, M2, P], U8, name="g_scales", align_bytes=64),
                 )
-            pairs = work.tile([P, 2, K_PASS], F32)
-            nc.vector.tensor_add(out=pairs[:], in0=squares[:, 0:2, :], in1=squares[:, 2:4, :])
-            total = work.tile([P, K_PASS], F32)
-            nc.vector.tensor_add(out=total[:], in0=pairs[:, 0, :], in1=pairs[:, 1, :])
-            nc.vector.tensor_add(out=total[:], in0=total[:], in1=squares[:, 4, :])
-            nc.vector.tensor_scalar_max(out=total[:], in0=total[:], scalar1=EPS * EPS)
-            nc.scalar.activation(out=inv_norm[:, fg, :], in_=total[:], func=ACT.Abs_reciprocal_sqrt)
-            nc.vector.tensor_mul(out=norm[:, fg, :], in0=total[:], in1=inv_norm[:, fg, :])
-
-        def gate_of_tile(inv_norm, norm, gate):
-            for fg in range(F_GROUPS):
-                for j in range(PACK):
-                    cols = slice(j * P, (j + 1) * P)
-                    c = fg * PACK + j
-                    nc.scalar.activation(
-                        out=gate[:, fg, cols],
-                        in_=norm[:, fg, cols],
-                        func=ACT.Gelu,
-                        scale=gain[:, c : c + 1],
-                        bias=shift[:, c : c + 1],
-                    )
-                nc.vector.tensor_mul(out=gate[:, fg, :], in0=gate[:, fg, :], in1=inv_norm[:, fg, :])
-
-        def gated_unit(tt, fg, gate, g_codes, g_scales):
-            g_grouped = work.tile([P, M2, P, PACK], BF16, align_bytes=64)
-            for m in range(M2):
-                h = psum_gate.tile([P, PACK, P], F32)
-                first_matmul(h, tt, fg, m)
-                nc.vector.tensor_tensor(
-                    out=g_grouped[:, m, :, :],
-                    in0=h[:].rearrange("p j t -> p t j"),
-                    in1=gate[:, fg, :].rearrange("p (j t) -> p t j", j=PACK),
-                    op=ALU.mult,
-                )
+            g_codes, g_scales = g_words_of[tt]
             for first, last in ((0, 4), (4, 5)):
                 nc.vector.quantize_mx(
                     out=g_codes[:, fg, first:last, :].rearrange("p m t -> p (m t)").bitcast(FP8X4),
                     scales=g_scales[:, fg, first:last, :].rearrange("p m t -> p (m t)"),
-                    in_=g_grouped[:, first:last, :, :].rearrange("p m t j -> p (m t j)"),
+                    in_=g_grouped_of[unit][:, first:last, :, :].rearrange("p m t j -> p (m t j)"),
                 )
 
-        def second_matmul(tt, g_codes, g_scales):
-            y_planes = per_tile.tile([P, M2, D], F32, tag="y_planes")
-            for m in range(M2):
-                y = psum_out.tile([P, D], F32)
-                for fg in range(F_GROUPS):
-                    nc.tensor.matmul_mx(
-                        out=y[:],
-                        lhsT=g_codes[:, fg, m, :].bitcast(FP8X4),
-                        lhsT_scale=g_scales[:, fg, m, :],
-                        rhs=w2_codes[:, fg, :].bitcast(FP8X4),
-                        rhs_scale=w2_scales[:, fg, :],
-                        start=(fg == 0),
-                        stop=(fg == F_GROUPS - 1),
-                    )
-                nc.scalar.copy(out=y_planes[:, m, :], in_=y[:])
-            y_rows = per_tile.tile([P, D, M2], F32, tag="y_rows")
+        def output_component(tt, m):
+            if m == 0:
+                y_planes_of[tt] = y_pool.tile([P, M2, D], F32, name="y_planes")
+            g_codes, g_scales = g_words_of[tt]
+            y = psum_out.tile([P, D], F32, tag="bank")
+            for fg in range(F_GROUPS):
+                nc.tensor.matmul_mx(
+                    out=y[:],
+                    lhsT=g_codes[:, fg, m, :].bitcast(FP8X4),
+                    lhsT_scale=g_scales[:, fg, m, :],
+                    rhs=w2_codes[:, fg, :].bitcast(FP8X4),
+                    rhs_scale=w2_scales[:, fg, :],
+                    start=(fg == 0),
+                    stop=(fg == F_GROUPS - 1),
+                )
+            nc.scalar.copy(out=y_planes_of[tt][:, m, :], in_=y[:])
+
+        def store_tile(tt):
+            half = D // 2
+            planes = y_planes_of[tt][:].rearrange("t m d -> t d m")
+            rows = out[tt].rearrange("n d m -> n (d m)")
+            y_low = pairs_of.tile([P, half, M2], F32, name="y_low")
+            nc.vector.tensor_copy(out=y_low[:], in_=planes[:, 0:half, :])
+            nc.sync.dma_start(
+                out=rows[:, 0 : half * M2], in_=y_low[:].rearrange("t d m -> t (d m)")
+            )
+            y_high = pairs_of.tile([P, half, M2], F32, name="y_high")
             nc.gpsimd.tensor_scalar(
-                out=y_rows[:],
-                in0=y_planes[:].rearrange("t m d -> t d m"),
+                out=y_high[:],
+                in0=planes[:, half:D, :],
                 scalar1=1.0,
                 scalar2=0.0,
                 op0=ALU.mult,
                 op1=ALU.add,
             )
             nc.sync.dma_start(
-                out=out[tt].rearrange("n d m -> n (d m)"), in_=y_rows[:].rearrange("t d m -> t (d m)")
+                out=rows[:, half * M2 : D * M2], in_=y_high[:].rearrange("t d m -> t (d m)")
             )
 
-        def new_norm_tiles():
-            inv_norm = chain.tile([P, F_GROUPS, K_PASS], F32, tag="inv_norm")
-            norm = chain.tile([P, F_GROUPS, K_PASS], F32, tag="norm")
-            return inv_norm, norm
-
-        gain_bf = consts.tile([P, F_GROUPS, PACK], BF16)
-        shift_bf = consts.tile([P, F_GROUPS, PACK], BF16)
-        by_partition = "a b (g p j) -> p (a b g) j"
-        nc.scalar.dma_start(out=gain_bf[:], in_=scale.rearrange(by_partition, p=P, j=PACK))
-        nc.scalar.dma_start(out=shift_bf[:], in_=bias.rearrange(by_partition, p=P, j=PACK))
-        gain = consts.tile([P, F_GROUPS * PACK], F32)
-        shift = consts.tile([P, F_GROUPS * PACK], F32)
+        x_sorted = sort_x(0)
+        quantise_w_in(0)
+        pack_x(0, x_sorted)
+        for fg in range(1, F_GROUPS):
+            quantise_w_in(fg)
         nc.vector.tensor_copy(out=gain[:], in_=gain_bf[:].rearrange("p g j -> p (g j)"))
         nc.vector.tensor_copy(out=shift[:], in_=shift_bf[:].rearrange("p g j -> p (g j)"))
 
-        quantise_x(0)
-        for fg in range(F_GROUPS):
-            quantise_w_in(fg)
-        inv_norm, norm = new_norm_tiles()
-        for fg in range(F_GROUPS):
-            norms_of_unit(0, fg, inv_norm, norm)
-        for fg in range(F_GROUPS):
-            quantise_w_out(fg)
-        gate = per_tile.tile([P, F_GROUPS, K_PASS], F32, tag="gate")
-        gate_of_tile(inv_norm, norm, gate)
+        for step in range(UNITS + LEAD + F_GROUPS + 1):
+            squared = step
+            summed = step - 1
+            rooted = step - 2
+            gated = step - LEAD
+            written = step - LEAD - F_GROUPS
+            stored = written - 1
 
-        for tt in range(TOKEN_TILES):
-            ahead = tt + 1 < TOKEN_TILES
-            g_codes = per_tile.tile([P, F_GROUPS, M2, P], U32, tag="g_codes", align_bytes=64)
-            g_scales = per_tile.tile([P, F_GROUPS, M2, P], U8, tag="g_scales", align_bytes=64)
-            if ahead:
-                quantise_x(tt + 1)
-                inv_norm, norm = new_norm_tiles()
-            for fg in range(F_GROUPS):
-                if ahead:
-                    norms_of_unit(tt + 1, fg, inv_norm, norm)
-                gated_unit(tt, fg, gate, g_codes, g_scales)
-            if ahead:
-                gate = per_tile.tile([P, F_GROUPS, K_PASS], F32, tag="gate")
-                gate_of_tile(inv_norm, norm, gate)
-            second_matmul(tt, g_codes, g_scales)
+            next_tile = step // F_GROUPS + 1
+            if next_tile < TOKEN_TILES and step % F_GROUPS == 0:
+                x_sorted = sort_x(next_tile)
+            if next_tile < TOKEN_TILES and step % F_GROUPS == 1:
+                pack_x(next_tile, x_sorted)
+            if step < F_GROUPS:
+                quantise_w_out(step)
+
+            gelu_step = 0 <= rooted < UNITS and rooted % F_GROUPS == F_GROUPS - 1
+            for m in range(M2):
+                if squared < UNITS:
+                    square_component(squared, m)
+                if gelu_step and m < F_GROUPS:
+                    gate_of_unit(rooted - (F_GROUPS - 1) + m)
+                if 0 <= gated < UNITS:
+                    gate_component(gated, m)
+                if 0 <= summed < UNITS and m == 1:
+                    sums = sum_squares(summed)
+                if 0 <= summed < UNITS and m == 3:
+                    clamp_sums(summed, sums)
+            if 0 <= gated < UNITS:
+                quantise_g(gated)
+            if 0 <= stored < UNITS and stored % F_GROUPS == F_GROUPS - 1:
+                store_tile(stored // F_GROUPS)
+            if 0 <= summed < UNITS:
+                norm_of_unit(summed)
+            if 0 <= written < UNITS:
+                tt, quarter = divmod(written, F_GROUPS)
+                output_component(tt, quarter)
+                if quarter == F_GROUPS - 1:
+                    output_component(tt, M2 - 1)

@@ -39,8 +39,7 @@ def tile_feedforwardse3_pb_kernel(tc, x, w_in, scale, bias, w_out, out):
         six_of = stack.enter_context(tc.tile_pool(name="six_of", bufs=6))
         y_pool = stack.enter_context(tc.tile_pool(name="y_pool", bufs=1))
         psum_norm = stack.enter_context(tc.psum_pool(name="psum_norm", bufs=3))
-        psum_sum = stack.enter_context(tc.psum_pool(name="psum_sum", bufs=1))
-        psum_gate = stack.enter_context(tc.psum_pool(name="psum_gate", bufs=2))
+        psum_gate = stack.enter_context(tc.psum_pool(name="psum_gate", bufs=3))
         psum_out = stack.enter_context(tc.psum_pool(name="psum_out", bufs=2))
         stack.enter_context(tc.manual_schedule())
 
@@ -142,41 +141,48 @@ def tile_feedforwardse3_pb_kernel(tc, x, w_in, scale, bias, w_out, out):
         g_words_of = {}
         y_planes_of = {}
 
-        def square_component(unit, m):
+        def first_matmul(h, unit, m):
             tt, fg = divmod(unit, F_GROUPS)
+            for j in range(PACK):
+                cols = slice(j * P, (j + 1) * P)
+                nc.tensor.matmul_mx(
+                    out=h[:, j, :],
+                    lhsT=w1_codes[:, fg, cols].bitcast(FP8X4),
+                    lhsT_scale=w1_scales[:, fg, cols],
+                    rhs=x_codes[:, tt, m, :].bitcast(FP8X4),
+                    rhs_scale=x_scales[:, tt, m, :],
+                    start=True,
+                    stop=True,
+                )
+
+        def square_component(unit, m):
             if m == 0:
                 squares_of[unit] = pairs_of.tile([P, M2, K_PASS], F32, name="squares")
-            h_rows = psum_norm.tile([P, K_PASS], F32)
-            nc.tensor.matmul_mx(
-                out=h_rows[:],
-                lhsT=x_codes[:, tt, m, :].bitcast(FP8X4),
-                lhsT_scale=x_scales[:, tt, m, :],
-                rhs=w1_codes[:, fg, :].bitcast(FP8X4),
-                rhs_scale=w1_scales[:, fg, :],
-                start=True,
-                stop=True,
+            h = psum_norm.tile([P, PACK, P], F32)
+            first_matmul(h, unit, m)
+            nc.scalar.activation(
+                out=squares_of[unit][:, m, :], in_=h[:].rearrange("p j t -> p (j t)"), func=ACT.Square
             )
-            nc.scalar.activation(out=squares_of[unit][:, m, :], in_=h_rows[:], func=ACT.Square)
 
-        def sum_squares(unit):
-            sums = psum_sum.tile([P, PACK, P], F32)
-            for j in range(PACK):
-                for m in range(M2):
-                    nc.tensor.matmul(
-                        out=sums[:, j, :],
-                        lhsT=squares_of[unit][:, m, j * P : (j + 1) * P],
-                        rhs=identity[:],
-                        is_transpose=True,
-                        start=(m == 0),
-                        stop=(m == M2 - 1),
-                    )
-            return sums
-
-        def clamp_sums(unit, sums):
-            total_of[unit] = pairs_of.tile([P, K_PASS], F32, name="total")
-            nc.vector.tensor_scalar_max(
-                out=total_of[unit][:], in0=sums[:].rearrange("p j t -> p (j t)"), scalar1=EPS * EPS
-            )
+        def sum_squares(unit, link):
+            squares = squares_of[unit]
+            if link == 0:
+                nc.vector.tensor_add(
+                    out=squares[:, 0:2, :], in0=squares[:, 0:2, :], in1=squares[:, 2:4, :]
+                )
+            if link == 1:
+                nc.vector.tensor_add(
+                    out=squares[:, 0, :], in0=squares[:, 0, :], in1=squares[:, 1, :]
+                )
+            if link == 2:
+                nc.vector.tensor_add(
+                    out=squares[:, 0, :], in0=squares[:, 0, :], in1=squares[:, 4, :]
+                )
+            if link == 3:
+                total_of[unit] = pairs_of.tile([P, K_PASS], F32, name="total")
+                nc.vector.tensor_scalar_max(
+                    out=total_of[unit][:], in0=squares[:, 0, :], scalar1=EPS * EPS
+                )
 
         def norm_of_unit(unit):
             inv_norm_of[unit] = six_of.tile([P, K_PASS], F32, name="inv_norm")
@@ -210,23 +216,12 @@ def tile_feedforwardse3_pb_kernel(tc, x, w_in, scale, bias, w_out, out):
             )
 
         def gate_component(unit, m):
-            tt, fg = divmod(unit, F_GROUPS)
             if m == 0:
                 g_grouped_of[unit] = pairs_of.tile(
                     [P, M2, P, PACK], BF16, name="g_grouped", align_bytes=64
                 )
             h = psum_gate.tile([P, PACK, P], F32)
-            for j in range(PACK):
-                cols = slice(j * P, (j + 1) * P)
-                nc.tensor.matmul_mx(
-                    out=h[:, j, :],
-                    lhsT=w1_codes[:, fg, cols].bitcast(FP8X4),
-                    lhsT_scale=w1_scales[:, fg, cols],
-                    rhs=x_codes[:, tt, m, :].bitcast(FP8X4),
-                    rhs_scale=x_scales[:, tt, m, :],
-                    start=True,
-                    stop=True,
-                )
+            first_matmul(h, unit, m)
             nc.vector.tensor_tensor(
                 out=g_grouped_of[unit][:, m, :, :],
                 in0=h[:].rearrange("p j t -> p t j"),
@@ -320,10 +315,8 @@ def tile_feedforwardse3_pb_kernel(tc, x, w_in, scale, bias, w_out, out):
                     gate_of_unit(rooted - (F_GROUPS - 1) + m)
                 if 0 <= gated < UNITS:
                     gate_component(gated, m)
-                if 0 <= summed < UNITS and m == 1:
-                    sums = sum_squares(summed)
-                if 0 <= summed < UNITS and m == 3:
-                    clamp_sums(summed, sums)
+                if 0 <= summed < UNITS and m < M2 - 1:
+                    sum_squares(summed, m)
             if 0 <= gated < UNITS:
                 quantise_g(gated)
             if 0 <= stored < UNITS and stored % F_GROUPS == F_GROUPS - 1:

@@ -39,10 +39,15 @@ def tile_feedforwardse3_pb_kernel(tc, x, w_in, scale, bias, w_out, out):
         six_of = stack.enter_context(tc.tile_pool(name="six_of", bufs=6))
         y_pool = stack.enter_context(tc.tile_pool(name="y_pool", bufs=1))
         psum_norm = stack.enter_context(tc.psum_pool(name="psum_norm", bufs=3))
-        psum_gate = stack.enter_context(tc.psum_pool(name="psum_gate", bufs=3))
+        psum_sum = stack.enter_context(tc.psum_pool(name="psum_sum", bufs=1))
+        psum_gate = stack.enter_context(tc.psum_pool(name="psum_gate", bufs=2))
         psum_out = stack.enter_context(tc.psum_pool(name="psum_out", bufs=2))
         stack.enter_context(tc.manual_schedule())
 
+        minus_eps2 = consts.tile([P, 1], F32)
+        plus_eps2 = consts.tile([P, 1], F32)
+        nc.vector.memset(minus_eps2[:], -EPS * EPS)
+        nc.vector.memset(plus_eps2[:], EPS * EPS)
         identity = consts.tile([P, P], F32)
         make_identity(nc, identity[:])
 
@@ -133,7 +138,7 @@ def tile_feedforwardse3_pb_kernel(tc, x, w_in, scale, bias, w_out, out):
             )
 
         squares_of = {}
-        total_of = {}
+        excess_of = {}
         inv_norm_of = {}
         norm_of = {}
         gate_of = {}
@@ -141,60 +146,64 @@ def tile_feedforwardse3_pb_kernel(tc, x, w_in, scale, bias, w_out, out):
         g_words_of = {}
         y_planes_of = {}
 
-        def first_matmul(h, unit, m):
-            tt, fg = divmod(unit, F_GROUPS)
-            for j in range(PACK):
-                cols = slice(j * P, (j + 1) * P)
-                nc.tensor.matmul_mx(
-                    out=h[:, j, :],
-                    lhsT=w1_codes[:, fg, cols].bitcast(FP8X4),
-                    lhsT_scale=w1_scales[:, fg, cols],
-                    rhs=x_codes[:, tt, m, :].bitcast(FP8X4),
-                    rhs_scale=x_scales[:, tt, m, :],
-                    start=True,
-                    stop=True,
-                )
-
         def square_component(unit, m):
+            tt, fg = divmod(unit, F_GROUPS)
             if m == 0:
                 squares_of[unit] = pairs_of.tile([P, M2, K_PASS], F32, name="squares")
-            h = psum_norm.tile([P, PACK, P], F32)
-            first_matmul(h, unit, m)
-            nc.scalar.activation(
-                out=squares_of[unit][:, m, :], in_=h[:].rearrange("p j t -> p (j t)"), func=ACT.Square
+            h_rows = psum_norm.tile([P, K_PASS], F32)
+            nc.tensor.matmul_mx(
+                out=h_rows[:],
+                lhsT=x_codes[:, tt, m, :].bitcast(FP8X4),
+                lhsT_scale=x_scales[:, tt, m, :],
+                rhs=w1_codes[:, fg, :].bitcast(FP8X4),
+                rhs_scale=w1_scales[:, fg, :],
+                start=True,
+                stop=True,
             )
+            nc.scalar.activation(out=squares_of[unit][:, m, :], in_=h_rows[:], func=ACT.Square)
 
-        def sum_squares(unit, link):
-            squares = squares_of[unit]
-            if link == 0:
-                nc.vector.tensor_add(
-                    out=squares[:, 0:2, :], in0=squares[:, 0:2, :], in1=squares[:, 2:4, :]
-                )
-            if link == 1:
-                nc.vector.tensor_add(
-                    out=squares[:, 0, :], in0=squares[:, 0, :], in1=squares[:, 1, :]
-                )
-            if link == 2:
-                nc.vector.tensor_add(
-                    out=squares[:, 0, :], in0=squares[:, 0, :], in1=squares[:, 4, :]
-                )
-            if link == 3:
-                total_of[unit] = pairs_of.tile([P, K_PASS], F32, name="total")
-                nc.vector.tensor_scalar_max(
-                    out=total_of[unit][:], in0=squares[:, 0, :], scalar1=EPS * EPS
-                )
+        def sum_squares(unit):
+            sums = psum_sum.tile([P, PACK, P], F32)
+            for j in range(PACK):
+                for m in range(M2):
+                    nc.tensor.matmul(
+                        out=sums[:, j, :],
+                        lhsT=squares_of[unit][:, m, j * P : (j + 1) * P],
+                        rhs=identity[:],
+                        is_transpose=True,
+                        start=(m == 0),
+                        stop=(m == M2 - 1),
+                    )
+            return sums
 
-        def norm_of_unit(unit):
+        def root_of_unit(unit, sums):
+            excess_of[unit] = six_of.tile([P, K_PASS], F32, name="excess")
             inv_norm_of[unit] = six_of.tile([P, K_PASS], F32, name="inv_norm")
-            norm_of[unit] = six_of.tile([P, K_PASS], F32, name="norm")
             nc.scalar.activation(
-                out=inv_norm_of[unit][:], in_=total_of[unit][:], func=ACT.Abs_reciprocal_sqrt
+                out=excess_of[unit][:],
+                in_=sums[:].rearrange("p j t -> p (j t)"),
+                func=ACT.Relu,
+                bias=minus_eps2[:],
             )
-            nc.gpsimd.tensor_tensor(
-                out=norm_of[unit][:], in0=total_of[unit][:], in1=inv_norm_of[unit][:], op=ALU.mult
+            nc.scalar.activation(
+                out=inv_norm_of[unit][:],
+                in_=excess_of[unit][:],
+                func=ACT.Abs_reciprocal_sqrt,
+                bias=plus_eps2[:],
             )
 
-        def gate_of_unit(unit):
+        def norm_mul(unit):
+            norm_of[unit] = six_of.tile([P, K_PASS], F32, name="norm")
+            nc.vector.scalar_tensor_tensor(
+                out=norm_of[unit][:],
+                in0=excess_of[unit][:],
+                scalar=EPS * EPS,
+                in1=inv_norm_of[unit][:],
+                op0=ALU.add,
+                op1=ALU.mult,
+            )
+
+        def gelu_of_unit(unit):
             fg = unit % F_GROUPS
             gelu = norm_of[unit]
             for j in range(PACK):
@@ -207,8 +216,11 @@ def tile_feedforwardse3_pb_kernel(tc, x, w_in, scale, bias, w_out, out):
                     scale=gain[:, c : c + 1],
                     bias=shift[:, c : c + 1],
                 )
+
+        def gate_mul(unit):
+            gelu = norm_of[unit]
             gate_of[unit] = six_of.tile([P, P, PACK], F32, name="gate")
-            nc.gpsimd.tensor_tensor(
+            nc.vector.tensor_tensor(
                 out=gate_of[unit][:],
                 in0=gelu[:].rearrange("p (j t) -> p t j", j=PACK),
                 in1=inv_norm_of[unit][:].rearrange("p (j t) -> p t j", j=PACK),
@@ -216,12 +228,23 @@ def tile_feedforwardse3_pb_kernel(tc, x, w_in, scale, bias, w_out, out):
             )
 
         def gate_component(unit, m):
+            tt, fg = divmod(unit, F_GROUPS)
             if m == 0:
                 g_grouped_of[unit] = pairs_of.tile(
                     [P, M2, P, PACK], BF16, name="g_grouped", align_bytes=64
                 )
             h = psum_gate.tile([P, PACK, P], F32)
-            first_matmul(h, unit, m)
+            for j in range(PACK):
+                cols = slice(j * P, (j + 1) * P)
+                nc.tensor.matmul_mx(
+                    out=h[:, j, :],
+                    lhsT=w1_codes[:, fg, cols].bitcast(FP8X4),
+                    lhsT_scale=w1_scales[:, fg, cols],
+                    rhs=x_codes[:, tt, m, :].bitcast(FP8X4),
+                    rhs_scale=x_scales[:, tt, m, :],
+                    start=True,
+                    stop=True,
+                )
             nc.vector.tensor_tensor(
                 out=g_grouped_of[unit][:, m, :, :],
                 in0=h[:].rearrange("p j t -> p t j"),
@@ -271,14 +294,7 @@ def tile_feedforwardse3_pb_kernel(tc, x, w_in, scale, bias, w_out, out):
                 out=rows[:, 0 : half * M2], in_=y_low[:].rearrange("t d m -> t (d m)")
             )
             y_high = pairs_of.tile([P, half, M2], F32, name="y_high")
-            nc.gpsimd.tensor_scalar(
-                out=y_high[:],
-                in0=planes[:, half:D, :],
-                scalar1=1.0,
-                scalar2=0.0,
-                op0=ALU.mult,
-                op1=ALU.add,
-            )
+            nc.scalar.copy(out=y_high[:], in_=planes[:, half:D, :])
             nc.sync.dma_start(
                 out=rows[:, half * M2 : D * M2], in_=y_high[:].rearrange("t d m -> t (d m)")
             )
@@ -288,8 +304,6 @@ def tile_feedforwardse3_pb_kernel(tc, x, w_in, scale, bias, w_out, out):
         pack_x(0, x_sorted)
         for fg in range(1, F_GROUPS):
             quantise_w_in(fg)
-        nc.vector.tensor_copy(out=gain[:], in_=gain_bf[:].rearrange("p g j -> p (g j)"))
-        nc.vector.tensor_copy(out=shift[:], in_=shift_bf[:].rearrange("p g j -> p (g j)"))
 
         for step in range(UNITS + LEAD + F_GROUPS + 1):
             squared = step
@@ -299,32 +313,37 @@ def tile_feedforwardse3_pb_kernel(tc, x, w_in, scale, bias, w_out, out):
             written = step - LEAD - F_GROUPS
             stored = written - 1
 
-            next_tile = step // F_GROUPS + 1
-            if next_tile < TOKEN_TILES and step % F_GROUPS == 0:
-                x_sorted = sort_x(next_tile)
-            if next_tile < TOKEN_TILES and step % F_GROUPS == 1:
-                pack_x(next_tile, x_sorted)
-            if step < F_GROUPS:
-                quantise_w_out(step)
-
             gelu_step = 0 <= rooted < UNITS and rooted % F_GROUPS == F_GROUPS - 1
             for m in range(M2):
                 if squared < UNITS:
                     square_component(squared, m)
+                if 0 <= rooted < UNITS and m == 0:
+                    norm_mul(rooted)
                 if gelu_step and m < F_GROUPS:
-                    gate_of_unit(rooted - (F_GROUPS - 1) + m)
+                    gelu_of_unit(rooted - (F_GROUPS - 1) + m)
+                if gelu_step and m >= 1:
+                    gate_mul(rooted - (F_GROUPS - 1) + m - 1)
                 if 0 <= gated < UNITS:
                     gate_component(gated, m)
-                if 0 <= summed < UNITS and m < M2 - 1:
-                    sum_squares(summed, m)
+                if 0 <= summed < UNITS and m == 1:
+                    sums = sum_squares(summed)
             if 0 <= gated < UNITS:
                 quantise_g(gated)
             if 0 <= stored < UNITS and stored % F_GROUPS == F_GROUPS - 1:
                 store_tile(stored // F_GROUPS)
             if 0 <= summed < UNITS:
-                norm_of_unit(summed)
+                root_of_unit(summed, sums)
             if 0 <= written < UNITS:
                 tt, quarter = divmod(written, F_GROUPS)
                 output_component(tt, quarter)
                 if quarter == F_GROUPS - 1:
                     output_component(tt, M2 - 1)
+            if 2 <= step < TOKEN_TILES + 1:
+                pack_x(step - 1, x_sorted)
+            if 1 <= step < TOKEN_TILES:
+                x_sorted = sort_x(step)
+            if step == 3:
+                nc.vector.tensor_copy(out=gain[:], in_=gain_bf[:].rearrange("p g j -> p (g j)"))
+                nc.vector.tensor_copy(out=shift[:], in_=shift_bf[:].rearrange("p g j -> p (g j)"))
+            if 4 <= step < 4 + F_GROUPS:
+                quantise_w_out(step - 4)

@@ -37,17 +37,13 @@ def tile_feedforwardse3_pb_kernel(tc, x, w_in, scale, bias, w_out, out):
         w_rows_pool = stack.enter_context(tc.tile_pool(name="w_rows_pool", bufs=4))
         pairs_of = stack.enter_context(tc.tile_pool(name="pairs_of", bufs=2))
         six_of = stack.enter_context(tc.tile_pool(name="six_of", bufs=6))
-        y_pool = stack.enter_context(tc.tile_pool(name="y_pool", bufs=1))
+        y_pool = stack.enter_context(tc.tile_pool(name="y_pool", bufs=2))
         psum_norm = stack.enter_context(tc.psum_pool(name="psum_norm", bufs=3))
         psum_sum = stack.enter_context(tc.psum_pool(name="psum_sum", bufs=1))
         psum_gate = stack.enter_context(tc.psum_pool(name="psum_gate", bufs=2))
         psum_out = stack.enter_context(tc.psum_pool(name="psum_out", bufs=2))
         stack.enter_context(tc.manual_schedule())
 
-        minus_eps2 = consts.tile([P, 1], F32)
-        plus_eps2 = consts.tile([P, 1], F32)
-        nc.vector.memset(minus_eps2[:], -EPS * EPS)
-        nc.vector.memset(plus_eps2[:], EPS * EPS)
         identity = consts.tile([P, P], F32)
         make_identity(nc, identity[:])
 
@@ -138,7 +134,7 @@ def tile_feedforwardse3_pb_kernel(tc, x, w_in, scale, bias, w_out, out):
             )
 
         squares_of = {}
-        excess_of = {}
+        total_of = {}
         inv_norm_of = {}
         norm_of = {}
         gate_of = {}
@@ -176,31 +172,22 @@ def tile_feedforwardse3_pb_kernel(tc, x, w_in, scale, bias, w_out, out):
                     )
             return sums
 
-        def root_of_unit(unit, sums):
-            excess_of[unit] = six_of.tile([P, K_PASS], F32, name="excess")
+        def clamp_sums(unit, sums):
+            total_of[unit] = six_of.tile([P, K_PASS], F32, name="total")
+            nc.vector.tensor_scalar_max(
+                out=total_of[unit][:], in0=sums[:].rearrange("p j t -> p (j t)"), scalar1=EPS * EPS
+            )
+
+        def root_of_unit(unit):
             inv_norm_of[unit] = six_of.tile([P, K_PASS], F32, name="inv_norm")
             nc.scalar.activation(
-                out=excess_of[unit][:],
-                in_=sums[:].rearrange("p j t -> p (j t)"),
-                func=ACT.Relu,
-                bias=minus_eps2[:],
-            )
-            nc.scalar.activation(
-                out=inv_norm_of[unit][:],
-                in_=excess_of[unit][:],
-                func=ACT.Abs_reciprocal_sqrt,
-                bias=plus_eps2[:],
+                out=inv_norm_of[unit][:], in_=total_of[unit][:], func=ACT.Abs_reciprocal_sqrt
             )
 
         def norm_mul(unit):
             norm_of[unit] = six_of.tile([P, K_PASS], F32, name="norm")
-            nc.vector.scalar_tensor_tensor(
-                out=norm_of[unit][:],
-                in0=excess_of[unit][:],
-                scalar=EPS * EPS,
-                in1=inv_norm_of[unit][:],
-                op0=ALU.add,
-                op1=ALU.mult,
+            nc.gpsimd.tensor_tensor(
+                out=norm_of[unit][:], in0=total_of[unit][:], in1=inv_norm_of[unit][:], op=ALU.mult
             )
 
         def gelu_of_unit(unit):
@@ -220,7 +207,7 @@ def tile_feedforwardse3_pb_kernel(tc, x, w_in, scale, bias, w_out, out):
         def gate_mul(unit):
             gelu = norm_of[unit]
             gate_of[unit] = six_of.tile([P, P, PACK], F32, name="gate")
-            nc.vector.tensor_tensor(
+            nc.gpsimd.tensor_tensor(
                 out=gate_of[unit][:],
                 in0=gelu[:].rearrange("p (j t) -> p t j", j=PACK),
                 in1=inv_norm_of[unit][:].rearrange("p (j t) -> p t j", j=PACK),
@@ -327,12 +314,14 @@ def tile_feedforwardse3_pb_kernel(tc, x, w_in, scale, bias, w_out, out):
                     gate_component(gated, m)
                 if 0 <= summed < UNITS and m == 1:
                     sums = sum_squares(summed)
+                if 0 <= summed < UNITS and m == 3:
+                    clamp_sums(summed, sums)
             if 0 <= gated < UNITS:
                 quantise_g(gated)
             if 0 <= stored < UNITS and stored % F_GROUPS == F_GROUPS - 1:
                 store_tile(stored // F_GROUPS)
             if 0 <= summed < UNITS:
-                root_of_unit(summed, sums)
+                root_of_unit(summed)
             if 0 <= written < UNITS:
                 tt, quarter = divmod(written, F_GROUPS)
                 output_component(tt, quarter)

@@ -22,7 +22,8 @@ UNITS = TOKEN_TILES * F_GROUPS
 M2 = 5
 EPS = 1e-12
 
-LEAD = 6
+GELU_BATCH = 2
+LEAD = GELU_BATCH + 2
 
 FLOPS = 2 * 2 * (TOKEN_TILES * P * M2) * D * F
 
@@ -36,7 +37,7 @@ def tile_feedforwardse3_pb_kernel(tc, x, w_in, scale, bias, w_out, out):
         x_work = stack.enter_context(tc.tile_pool(name="x_work", bufs=1))
         w_rows_pool = stack.enter_context(tc.tile_pool(name="w_rows_pool", bufs=4))
         pairs_of = stack.enter_context(tc.tile_pool(name="pairs_of", bufs=2))
-        six_of = stack.enter_context(tc.tile_pool(name="six_of", bufs=6))
+        two_batches = stack.enter_context(tc.tile_pool(name="two_batches", bufs=2 * GELU_BATCH))
         y_pool = stack.enter_context(tc.tile_pool(name="y_pool", bufs=2))
         psum_norm = stack.enter_context(tc.psum_pool(name="psum_norm", bufs=3))
         psum_sum = stack.enter_context(tc.psum_pool(name="psum_sum", bufs=1))
@@ -88,7 +89,7 @@ def tile_feedforwardse3_pb_kernel(tc, x, w_in, scale, bias, w_out, out):
             )
             return x_sorted
 
-        def pack_x(tt, x_sorted):
+        def pack_x(tt, x_sorted, copy_out):
             x_pairs = x_sorted[:].bitcast(F32)
             x_grouped = x_work.tile([P, M2, K_PASS], BF16, name="x_grouped", align_bytes=64)
             for first in range(0, M2, 2):
@@ -99,7 +100,7 @@ def tile_feedforwardse3_pb_kernel(tc, x, w_in, scale, bias, w_out, out):
                     nc.tensor.transpose(
                         x_t[:, i // 2, i % 2, :], x_pairs[:, start : start + P], identity[:]
                     )
-                nc.vector.tensor_copy(
+                copy_out(
                     out=x_grouped[:, first : first + count, :]
                     .rearrange("p m k -> p (m k)")
                     .bitcast(F32)
@@ -173,19 +174,19 @@ def tile_feedforwardse3_pb_kernel(tc, x, w_in, scale, bias, w_out, out):
             return sums
 
         def clamp_sums(unit, sums):
-            total_of[unit] = six_of.tile([P, K_PASS], F32, name="total")
+            total_of[unit] = two_batches.tile([P, K_PASS], F32, name="total")
             nc.vector.tensor_scalar_max(
                 out=total_of[unit][:], in0=sums[:].rearrange("p j t -> p (j t)"), scalar1=EPS * EPS
             )
 
         def root_of_unit(unit):
-            inv_norm_of[unit] = six_of.tile([P, K_PASS], F32, name="inv_norm")
+            inv_norm_of[unit] = two_batches.tile([P, K_PASS], F32, name="inv_norm")
             nc.scalar.activation(
                 out=inv_norm_of[unit][:], in_=total_of[unit][:], func=ACT.Abs_reciprocal_sqrt
             )
 
         def norm_mul(unit):
-            norm_of[unit] = six_of.tile([P, K_PASS], F32, name="norm")
+            norm_of[unit] = two_batches.tile([P, K_PASS], F32, name="norm")
             nc.gpsimd.tensor_tensor(
                 out=norm_of[unit][:], in0=total_of[unit][:], in1=inv_norm_of[unit][:], op=ALU.mult
             )
@@ -206,7 +207,7 @@ def tile_feedforwardse3_pb_kernel(tc, x, w_in, scale, bias, w_out, out):
 
         def gate_mul(unit):
             gelu = norm_of[unit]
-            gate_of[unit] = six_of.tile([P, P, PACK], F32, name="gate")
+            gate_of[unit] = two_batches.tile([P, P, PACK], F32, name="gate")
             nc.gpsimd.tensor_tensor(
                 out=gate_of[unit][:],
                 in0=gelu[:].rearrange("p (j t) -> p t j", j=PACK),
@@ -281,14 +282,21 @@ def tile_feedforwardse3_pb_kernel(tc, x, w_in, scale, bias, w_out, out):
                 out=rows[:, 0 : half * M2], in_=y_low[:].rearrange("t d m -> t (d m)")
             )
             y_high = pairs_of.tile([P, half, M2], F32, name="y_high")
-            nc.scalar.copy(out=y_high[:], in_=planes[:, half:D, :])
+            nc.gpsimd.tensor_scalar(
+                out=y_high[:],
+                in0=planes[:, half:D, :],
+                scalar1=1.0,
+                scalar2=0.0,
+                op0=ALU.mult,
+                op1=ALU.add,
+            )
             nc.sync.dma_start(
                 out=rows[:, half * M2 : D * M2], in_=y_high[:].rearrange("t d m -> t (d m)")
             )
 
         x_sorted = sort_x(0)
         quantise_w_in(0)
-        pack_x(0, x_sorted)
+        pack_x(0, x_sorted, nc.scalar.copy)
         for fg in range(1, F_GROUPS):
             quantise_w_in(fg)
 
@@ -300,16 +308,17 @@ def tile_feedforwardse3_pb_kernel(tc, x, w_in, scale, bias, w_out, out):
             written = step - LEAD - F_GROUPS
             stored = written - 1
 
-            gelu_step = 0 <= rooted < UNITS and rooted % F_GROUPS == F_GROUPS - 1
+            gelu_step = 0 <= rooted < UNITS and rooted % GELU_BATCH == GELU_BATCH - 1
+            batch_start = rooted - (GELU_BATCH - 1)
             for m in range(M2):
                 if squared < UNITS:
                     square_component(squared, m)
                 if 0 <= rooted < UNITS and m == 0:
                     norm_mul(rooted)
-                if gelu_step and m < F_GROUPS:
-                    gelu_of_unit(rooted - (F_GROUPS - 1) + m)
-                if gelu_step and m >= 1:
-                    gate_mul(rooted - (F_GROUPS - 1) + m - 1)
+                if gelu_step and m < GELU_BATCH:
+                    gelu_of_unit(batch_start + m)
+                if gelu_step and 1 <= m <= GELU_BATCH:
+                    gate_mul(batch_start + m - 1)
                 if 0 <= gated < UNITS:
                     gate_component(gated, m)
                 if 0 <= summed < UNITS and m == 1:
@@ -328,10 +337,10 @@ def tile_feedforwardse3_pb_kernel(tc, x, w_in, scale, bias, w_out, out):
                 if quarter == F_GROUPS - 1:
                     output_component(tt, M2 - 1)
             if 2 <= step < TOKEN_TILES + 1:
-                pack_x(step - 1, x_sorted)
+                pack_x(step - 1, x_sorted, nc.vector.tensor_copy)
             if 1 <= step < TOKEN_TILES:
                 x_sorted = sort_x(step)
-            if step == 3:
+            if step == 1:
                 nc.vector.tensor_copy(out=gain[:], in_=gain_bf[:].rearrange("p g j -> p (g j)"))
                 nc.vector.tensor_copy(out=shift[:], in_=shift_bf[:].rearrange("p g j -> p (g j)"))
             if 4 <= step < 4 + F_GROUPS:

@@ -84,8 +84,8 @@ def tile_feedforwardse3_pb_kernel(tc, x, w_in, scale, bias, w_out, out):
         def sort_x(tt):
             x_sorted = x_work.tile([P, M2 * D], BF16, name="x_sorted")
             nc.vector.tensor_copy(
-                out=x_sorted[:].rearrange("t (m u p e) -> t m u p e", m=M2, u=2, p=P, e=2),
-                in_=x_rows_of[tt][:].rearrange("t (p u e m) -> t m u p e", p=P, u=2, e=2, m=M2),
+                out=x_sorted[:].rearrange("t (m u p e) -> t u m p e", m=M2, u=2, p=P, e=2),
+                in_=x_rows_of[tt][:].rearrange("t (p u e m) -> t u m p e", p=P, u=2, e=2, m=M2),
             )
             return x_sorted
 

@@ -40,8 +40,7 @@ def tile_feedforwardse3_pb_kernel(tc, x, w_in, scale, bias, w_out, out):
         two_batches = stack.enter_context(tc.tile_pool(name="two_batches", bufs=2 * GELU_BATCH))
         y_pool = stack.enter_context(tc.tile_pool(name="y_pool", bufs=2))
         psum_norm = stack.enter_context(tc.psum_pool(name="psum_norm", bufs=3))
-        psum_sum = stack.enter_context(tc.psum_pool(name="psum_sum", bufs=1))
-        psum_gate = stack.enter_context(tc.psum_pool(name="psum_gate", bufs=2))
+        psum_gate = stack.enter_context(tc.psum_pool(name="psum_gate", bufs=3))
         psum_out = stack.enter_context(tc.psum_pool(name="psum_out", bufs=2))
         stack.enter_context(tc.manual_schedule())
 
@@ -160,7 +159,7 @@ def tile_feedforwardse3_pb_kernel(tc, x, w_in, scale, bias, w_out, out):
             nc.scalar.activation(out=squares_of[unit][:, m, :], in_=h_rows[:], func=ACT.Square)
 
         def sum_squares(unit):
-            sums = psum_sum.tile([P, PACK, P], F32)
+            sums = psum_out.tile([P, PACK, P], F32, tag="bank")
             for j in range(PACK):
                 for m in range(M2):
                     nc.tensor.matmul(

@@ -19,9 +19,12 @@ D = 512
 F = 2048
 F_GROUPS = F // K_PASS
 UNITS = TOKEN_TILES * F_GROUPS
+RUN = 4
 M2 = 5
 EPS = 1e-12
 
+SUM_PARTS = {1: (0, 2), 2: (2, 4)}
+CLAMP_M = 3
 GELU_BATCH = 2
 LEAD = GELU_BATCH + 2
 
@@ -158,9 +161,8 @@ def tile_feedforwardse3_pb_kernel(tc, x, w_in, scale, bias, w_out, out):
             )
             nc.scalar.activation(out=squares_of[unit][:, m, :], in_=h_rows[:], func=ACT.Square)
 
-        def sum_squares(unit):
-            sums = psum_out.tile([P, PACK, P], F32, tag="bank")
-            for j in range(PACK):
+        def sum_squares(unit, sums, first, last):
+            for j in range(first, last):
                 for m in range(M2):
                     nc.tensor.matmul(
                         out=sums[:, j, :],
@@ -170,7 +172,6 @@ def tile_feedforwardse3_pb_kernel(tc, x, w_in, scale, bias, w_out, out):
                         start=(m == 0),
                         stop=(m == M2 - 1),
                     )
-            return sums
 
         def clamp_sums(unit, sums):
             total_of[unit] = two_batches.tile([P, K_PASS], F32, name="total")
@@ -206,11 +207,11 @@ def tile_feedforwardse3_pb_kernel(tc, x, w_in, scale, bias, w_out, out):
 
         def gate_mul(unit):
             gelu = norm_of[unit]
-            gate_of[unit] = two_batches.tile([P, P, PACK], F32, name="gate")
+            gate_of[unit] = two_batches.tile([P, P // RUN, PACK, RUN], F32, name="gate")
             nc.gpsimd.tensor_tensor(
                 out=gate_of[unit][:],
-                in0=gelu[:].rearrange("p (j t) -> p t j", j=PACK),
-                in1=inv_norm_of[unit][:].rearrange("p (j t) -> p t j", j=PACK),
+                in0=gelu[:].rearrange("p (j q i) -> p q j i", j=PACK, i=RUN),
+                in1=inv_norm_of[unit][:].rearrange("p (j q i) -> p q j i", j=PACK, i=RUN),
                 op=ALU.mult,
             )
 
@@ -233,8 +234,8 @@ def tile_feedforwardse3_pb_kernel(tc, x, w_in, scale, bias, w_out, out):
                     stop=True,
                 )
             nc.vector.tensor_tensor(
-                out=g_grouped_of[unit][:, m, :, :],
-                in0=h[:].rearrange("p j t -> p t j"),
+                out=g_grouped_of[unit][:, m, :, :].rearrange("p (q i) j -> p q j i", i=RUN),
+                in0=h[:].rearrange("p j (q i) -> p q j i", i=RUN),
                 in1=gate_of[unit][:],
                 op=ALU.mult,
             )
@@ -320,9 +321,11 @@ def tile_feedforwardse3_pb_kernel(tc, x, w_in, scale, bias, w_out, out):
                     gate_mul(batch_start + m - 1)
                 if 0 <= gated < UNITS:
                     gate_component(gated, m)
-                if 0 <= summed < UNITS and m == 1:
-                    sums = sum_squares(summed)
-                if 0 <= summed < UNITS and m == 3:
+                if 0 <= summed < UNITS and m in SUM_PARTS:
+                    if SUM_PARTS[m][0] == 0:
+                        sums = psum_out.tile([P, PACK, P], F32, tag="bank")
+                    sum_squares(summed, sums, *SUM_PARTS[m])
+                if 0 <= summed < UNITS and m == CLAMP_M:
                     clamp_sums(summed, sums)
             if 0 <= gated < UNITS:
                 quantise_g(gated)

@@ -19,7 +19,7 @@ D = 512
 F = 2048
 F_GROUPS = F // K_PASS
 UNITS = TOKEN_TILES * F_GROUPS
-RUN = 4
+RUN = 2
 M2 = 5
 EPS = 1e-12
 

@@ -23,8 +23,24 @@ RUN = 2
 M2 = 5
 EPS = 1e-12
 
-SUM_PARTS = {1: (0, 2), 2: (2, 4)}
-CLAMP_M = 3
+SUM_PARTS = {1: (0, 4)}
+CLAMP_M = 2
+D_CLAMP = 1
+D_SUM = 0
+D_GELU = 3
+OUT_M = (2, 4)
+ROOT_LATE = 1
+AHEAD = 1
+X_PARTS = 3
+OUTS = (1, 1, 1, 2)
+X_FIRST = 2
+X_LATE = 3
+SORT_X = {1: 1, 2: 2, 3: 3}
+TURN_X = {2: 1, 3: 2, 4: 3}
+W_OUT = {4: 0, 5: 1, 6: 2, 7: 3}
+V_OUT = 1
+V_COPIES = (2, 4)
+STORE_S = 1
 GELU_BATCH = 2
 LEAD = GELU_BATCH + 2
 
@@ -91,25 +107,34 @@ def tile_feedforwardse3_pb_kernel(tc, x, w_in, scale, bias, w_out, out):
             )
             return x_sorted
 
-        def pack_x(tt, x_sorted, copy_out):
+        x_grouped_of = {}
+        x_banks_of = {}
+
+        def turn_x(tt, x_sorted, part):
             x_pairs = x_sorted[:].bitcast(F32)
-            x_grouped = x_work.tile([P, M2, K_PASS], BF16, name="x_grouped", align_bytes=64)
-            for first in range(0, M2, 2):
-                count = min(2, M2 - first)
-                x_t = psum_out.tile([P, 2, 2, P], F32, tag="bank")
-                for i in range(2 * count):
-                    start = (2 * first + i) * P
-                    nc.tensor.transpose(
-                        x_t[:, i // 2, i % 2, :], x_pairs[:, start : start + P], identity[:]
-                    )
-                copy_out(
-                    out=x_grouped[:, first : first + count, :]
-                    .rearrange("p m k -> p (m k)")
-                    .bitcast(F32)
-                    .rearrange("p (m t u) -> p m t u", m=count, u=2),
-                    in_=x_t[:, 0:count, :, :].rearrange("p m u t -> p m t u"),
+            x_t = psum_out.tile([P, 2, 2, P], F32, tag="bank")
+            x_banks_of[tt, part] = x_t
+            for i in range(2 * min(2, M2 - 2 * part)):
+                start = (4 * part + i) * P
+                nc.tensor.transpose(
+                    x_t[:, i // 2, i % 2, :], x_pairs[:, start : start + P], identity[:]
                 )
-            for m in range(M2):
+
+        def group_x(tt, part, copy_out):
+            if part == 0:
+                x_grouped = x_work.tile([P, M2, K_PASS], BF16, name="x_grouped", align_bytes=64)
+                x_grouped_of[tt] = x_grouped
+            x_grouped = x_grouped_of[tt]
+            first = 2 * part
+            count = min(2, M2 - first)
+            copy_out(
+                out=x_grouped[:, first : first + count, :]
+                .rearrange("p m k -> p (m k)")
+                .bitcast(F32)
+                .rearrange("p (m t u) -> p m t u", m=count, u=2),
+                in_=x_banks_of[tt, part][:, 0:count, :, :].rearrange("p m u t -> p m t u"),
+            )
+            for m in range(first, first + count):
                 nc.vector.quantize_mx(
                     out=x_codes[:, tt, m, :].bitcast(FP8X4),
                     scales=x_scales[:, tt, m, :],
@@ -143,6 +168,7 @@ def tile_feedforwardse3_pb_kernel(tc, x, w_in, scale, bias, w_out, out):
         gate_of = {}
         g_grouped_of = {}
         g_words_of = {}
+        y_of = {}
         y_planes_of = {}
 
         def square_component(unit, m):
@@ -240,7 +266,7 @@ def tile_feedforwardse3_pb_kernel(tc, x, w_in, scale, bias, w_out, out):
                 op=ALU.mult,
             )
 
-        def quantise_g(unit):
+        def quantise_g(unit, pieces=((0, 4), (4, 5))):
             tt, fg = divmod(unit, F_GROUPS)
             if fg == 0:
                 g_words_of[tt] = (
@@ -248,21 +274,27 @@ def tile_feedforwardse3_pb_kernel(tc, x, w_in, scale, bias, w_out, out):
                     pairs_of.tile([P, F_GROUPS, M2, P], U8, name="g_scales", align_bytes=64),
                 )
             g_codes, g_scales = g_words_of[tt]
-            for first, last in ((0, 4), (4, 5)):
+            for first, last in pieces:
                 nc.vector.quantize_mx(
                     out=g_codes[:, fg, first:last, :].rearrange("p m t -> p (m t)").bitcast(FP8X4),
                     scales=g_scales[:, fg, first:last, :].rearrange("p m t -> p (m t)"),
                     in_=g_grouped_of[unit][:, first:last, :, :].rearrange("p m t j -> p (m t j)"),
                 )
 
-        def output_component(tt, m):
-            if m == 0:
-                y_planes_of[tt] = y_pool.tile([P, M2, D], F32, name="y_planes")
+        def output_passes(tt, m, first, last):
+            if first == 0:
+                if m == 0:
+                    y_planes_of[tt] = y_pool.tile([P, M2, D], F32, name="y_planes")
+                if tt == TOKEN_TILES - 1 and m < 3:
+                    h_rows = psum_norm.tile([P, D], F32)
+                    y_of[tt, m] = h_rows
+                else:
+                    y = psum_out.tile([P, D], F32, tag="bank")
+                    y_of[tt, m] = y
             g_codes, g_scales = g_words_of[tt]
-            y = psum_out.tile([P, D], F32, tag="bank")
-            for fg in range(F_GROUPS):
+            for fg in range(first, last):
                 nc.tensor.matmul_mx(
-                    out=y[:],
+                    out=y_of[tt, m][:],
                     lhsT=g_codes[:, fg, m, :].bitcast(FP8X4),
                     lhsT_scale=g_scales[:, fg, m, :],
                     rhs=w2_codes[:, fg, :].bitcast(FP8X4),
@@ -270,80 +302,141 @@ def tile_feedforwardse3_pb_kernel(tc, x, w_in, scale, bias, w_out, out):
                     start=(fg == 0),
                     stop=(fg == F_GROUPS - 1),
                 )
-            nc.scalar.copy(out=y_planes_of[tt][:, m, :], in_=y[:])
+
+        def output_copy(tt, m, copy):
+            copy(out=y_planes_of[tt][:, m, :], in_=y_of[tt, m][:])
 
         def store_tile(tt):
             half = D // 2
             planes = y_planes_of[tt][:].rearrange("t m d -> t d m")
             rows = out[tt].rearrange("n d m -> n (d m)")
+            if tt == TOKEN_TILES - 2 and STORE_S:
+                copy_low = copy_high = nc.scalar.copy
+            elif tt == TOKEN_TILES - 1:
+                copy_low = copy_high = nc.vector.tensor_copy
+            else:
+                copy_low = nc.vector.tensor_copy
+                copy_high = None
             y_low = pairs_of.tile([P, half, M2], F32, name="y_low")
-            nc.vector.tensor_copy(out=y_low[:], in_=planes[:, 0:half, :])
+            copy_low(out=y_low[:], in_=planes[:, 0:half, :])
             nc.sync.dma_start(
                 out=rows[:, 0 : half * M2], in_=y_low[:].rearrange("t d m -> t (d m)")
             )
             y_high = pairs_of.tile([P, half, M2], F32, name="y_high")
-            nc.gpsimd.tensor_scalar(
-                out=y_high[:],
-                in0=planes[:, half:D, :],
-                scalar1=1.0,
-                scalar2=0.0,
-                op0=ALU.mult,
-                op1=ALU.add,
-            )
+            if copy_high:
+                copy_high(out=y_high[:], in_=planes[:, half:D, :])
+            else:
+                nc.gpsimd.tensor_scalar(
+                    out=y_high[:],
+                    in0=planes[:, half:D, :],
+                    scalar1=1.0,
+                    scalar2=0.0,
+                    op0=ALU.mult,
+                    op1=ALU.add,
+                )
             nc.sync.dma_start(
                 out=rows[:, half * M2 : D * M2], in_=y_high[:].rearrange("t d m -> t (d m)")
             )
 
         x_sorted = sort_x(0)
         quantise_w_in(0)
-        pack_x(0, x_sorted, nc.scalar.copy)
+        for part in range(X_PARTS):
+            turn_x(0, x_sorted, part)
+            group_x(0, part, nc.scalar.copy)
         for fg in range(1, F_GROUPS):
             quantise_w_in(fg)
 
-        for step in range(UNITS + LEAD + F_GROUPS + 1):
+        last = TOKEN_TILES - 1
+        outs = []
+        written = None
+        for step in range(UNITS + LEAD):
             squared = step
             summed = step - 1
             rooted = step - 2
             gated = step - LEAD
-            written = step - LEAD - F_GROUPS
-            stored = written - 1
+            drain = step == UNITS
 
-            gelu_step = 0 <= rooted < UNITS and rooted % GELU_BATCH == GELU_BATCH - 1
+            gelu_step = 0 <= rooted < UNITS - 1 and rooted % GELU_BATCH == GELU_BATCH - 1
             batch_start = rooted - (GELU_BATCH - 1)
             for m in range(M2):
-                if squared < UNITS:
-                    square_component(squared, m)
-                if 0 <= rooted < UNITS and m == 0:
+                if squared < UNITS and not (step == 0 and m == 0):
+                    for beat in range(M2 * step + m + AHEAD, M2 * step + m + AHEAD + 1):
+                        if beat < M2 * UNITS:
+                            square_component(*divmod(beat, M2))
+                if step == 0 and m == 0:
+                    for beat in range(AHEAD + 1):
+                        square_component(0, beat)
+                if 0 <= rooted < UNITS - 1 and m == 0:
                     norm_mul(rooted)
                 if gelu_step and m < GELU_BATCH:
                     gelu_of_unit(batch_start + m)
                 if gelu_step and 1 <= m <= GELU_BATCH:
                     gate_mul(batch_start + m - 1)
+                if drain and m == D_GELU:
+                    for unit in range(UNITS - GELU_BATCH, UNITS):
+                        gelu_of_unit(unit)
+                        gate_mul(unit)
                 if 0 <= gated < UNITS:
                     gate_component(gated, m)
-                if 0 <= summed < UNITS and m in SUM_PARTS:
+                if gated == UNITS - 1 and m:
+                    quantise_g(gated, ((m - 1, m),))
+                if drain and m == D_SUM:
+                    h_rows = psum_norm.tile([P, PACK, P], F32)
+                    sums = h_rows
+                    sum_squares(summed, sums, 0, PACK)
+                if 0 <= summed < UNITS and m in SUM_PARTS and not drain:
                     if SUM_PARTS[m][0] == 0:
                         sums = psum_out.tile([P, PACK, P], F32, tag="bank")
                     sum_squares(summed, sums, *SUM_PARTS[m])
-                if 0 <= summed < UNITS and m == CLAMP_M:
+                if 0 <= summed < UNITS and m == (D_CLAMP if drain else CLAMP_M):
                     clamp_sums(summed, sums)
-            if 0 <= gated < UNITS:
+                    if drain:
+                        root_of_unit(summed)
+                        norm_mul(summed)
+                if step in TURN_X:
+                    if 0 <= m - X_LATE < X_PARTS:
+                        group_x(TURN_X[step], m - X_LATE, nc.vector.tensor_copy)
+                    if 0 <= m - X_FIRST < X_PARTS:
+                        turn_x(TURN_X[step], x_sorted, m - X_FIRST)
+                if step >= UNITS and outs and m in OUT_M:
+                    output_passes(*outs[0], 0, F_GROUPS)
+                    output_copy(*outs.pop(0), nc.scalar.copy)
+                    if not outs:
+                        store_tile(last - 1)
+                if gated == UNITS - 2:
+                    output_passes(last, m, 0, F_GROUPS - 2)
+                if gated == UNITS - 1:
+                    output_passes(last, m, F_GROUPS - 2, F_GROUPS - 1)
+            if 0 <= gated < UNITS - 1:
                 quantise_g(gated)
-            if 0 <= stored < UNITS and stored % F_GROUPS == F_GROUPS - 1:
-                store_tile(stored // F_GROUPS)
-            if 0 <= summed < UNITS:
+                if written is not None:
+                    store_tile(written)
+                    written = None
+            elif gated == UNITS - 1:
+                quantise_g(gated, ((M2 - 1, M2),))
+            if 0 <= summed < UNITS and not drain and not ROOT_LATE:
                 root_of_unit(summed)
-            if 0 <= written < UNITS:
-                tt, quarter = divmod(written, F_GROUPS)
-                output_component(tt, quarter)
-                if quarter == F_GROUPS - 1:
-                    output_component(tt, M2 - 1)
-            if 2 <= step < TOKEN_TILES + 1:
-                pack_x(step - 1, x_sorted, nc.vector.tensor_copy)
-            if 1 <= step < TOKEN_TILES:
-                x_sorted = sort_x(step)
+            if step < UNITS and outs:
+                for i in range(OUTS[step % F_GROUPS]):
+                    if outs:
+                        output_passes(*outs[0], 0, F_GROUPS)
+                        output_copy(*outs.pop(0), nc.vector.tensor_copy if V_OUT else nc.scalar.copy)
+                if not outs:
+                    written = gated // F_GROUPS - 1
+            if 0 <= summed < UNITS and not drain and ROOT_LATE:
+                root_of_unit(summed)
+            if 0 <= gated < UNITS - F_GROUPS and gated % F_GROUPS == F_GROUPS - 1:
+                outs = [(gated // F_GROUPS, m) for m in range(M2)]
+            if step in TURN_X and X_LATE + X_PARTS > M2:
+                group_x(TURN_X[step], X_PARTS - 1, nc.vector.tensor_copy)
+            if step in SORT_X:
+                x_sorted = sort_x(SORT_X[step])
             if step == 1:
                 nc.vector.tensor_copy(out=gain[:], in_=gain_bf[:].rearrange("p g j -> p (g j)"))
                 nc.vector.tensor_copy(out=shift[:], in_=shift_bf[:].rearrange("p g j -> p (g j)"))
-            if 4 <= step < 4 + F_GROUPS:
-                quantise_w_out(step - 4)
+            if step in W_OUT:
+                quantise_w_out(W_OUT[step])
+        for m in range(M2):
+            output_passes(last, m, F_GROUPS - 1, F_GROUPS)
+            output_copy(last, m, nc.vector.tensor_copy if m in V_COPIES else nc.scalar.copy)
+        store_tile(last)

@@ -31,6 +31,11 @@ D_GELU = 3
 OUT_M = (2, 4)
 ROOT_LATE = 1
 AHEAD = 1
+HEAD1 = (0, 1, 2)
+HEAD2 = ()
+WG = 1
+GROUP_M2 = {}
+GROUP_W = {3: 0, 4: 1, 5: 2, 6: 3}
 X_PARTS = 3
 OUTS = (1, 1, 1, 2)
 X_FIRST = 2
@@ -99,13 +104,18 @@ def tile_feedforwardse3_pb_kernel(tc, x, w_in, scale, bias, w_out, out):
         gain = consts.tile([P, F_GROUPS * PACK], F32)
         shift = consts.tile([P, F_GROUPS * PACK], F32)
 
-        def sort_x(tt):
-            x_sorted = x_work.tile([P, M2 * D], BF16, name="x_sorted")
+        def sort_x(tt, x_sorted, first, last):
             nc.vector.tensor_copy(
-                out=x_sorted[:].rearrange("t (m u p e) -> t u m p e", m=M2, u=2, p=P, e=2),
-                in_=x_rows_of[tt][:].rearrange("t (p u e m) -> t u m p e", p=P, u=2, e=2, m=M2),
+                out=x_sorted[:].rearrange("t (m u p e) -> t u m p e", m=M2, u=2, p=P, e=2)[
+                    :, :, first:last, :, :
+                ],
+                in_=x_rows_of[tt][:].rearrange("t (p u e m) -> t u m p e", p=P, u=2, e=2, m=M2)[
+                    :, :, first:last, :, :
+                ],
             )
-            return x_sorted
+
+        def new_sorted():
+            return x_work.tile([P, M2 * D], BF16, name="x_sorted")
 
         x_grouped_of = {}
         x_banks_of = {}
@@ -152,15 +162,31 @@ def tile_feedforwardse3_pb_kernel(tc, x, w_in, scale, bias, w_out, out):
             )
 
         def quantise_w_out(fg):
-            w_grouped = pairs_of.tile([P, D * PACK], BF16, name="w_grouped", align_bytes=64)
-            nc.vector.tensor_copy(
-                out=w_grouped[:].rearrange("p (d j) -> p d j", j=PACK),
-                in_=w_out_rows[fg][:].rearrange("p j d -> p d j"),
-            )
             nc.vector.quantize_mx(
-                out=w2_codes[:, fg, :].bitcast(FP8X4), scales=w2_scales[:, fg, :], in_=w_grouped[:]
+                out=w2_codes[:, fg, :].bitcast(FP8X4),
+                scales=w2_scales[:, fg, :],
+                in_=w_out_grouped[fg][:],
             )
 
+        def group_w_out(fg):
+            w_grouped = pairs_of.tile([P, D * PACK], BF16, name="w_grouped", align_bytes=64)
+            w_out_grouped[fg] = w_grouped
+            if WG:
+                nc.gpsimd.tensor_scalar(
+                    out=w_grouped[:].rearrange("p (d j) -> p d j", j=PACK),
+                    in0=w_out_rows[fg][:].rearrange("p j d -> p d j"),
+                    scalar1=1.0,
+                    scalar2=0.0,
+                    op0=ALU.mult,
+                    op1=ALU.add,
+                )
+            else:
+                nc.vector.tensor_copy(
+                    out=w_grouped[:].rearrange("p (d j) -> p d j", j=PACK),
+                    in_=w_out_rows[fg][:].rearrange("p j d -> p d j"),
+                )
+
+        w_out_grouped = {}
         squares_of = {}
         total_of = {}
         inv_norm_of = {}
@@ -338,8 +364,12 @@ def tile_feedforwardse3_pb_kernel(tc, x, w_in, scale, bias, w_out, out):
                 out=rows[:, half * M2 : D * M2], in_=y_high[:].rearrange("t d m -> t (d m)")
             )
 
-        x_sorted = sort_x(0)
+        x_sorted = new_sorted()
+        for part in HEAD1:
+            sort_x(0, x_sorted, 2 * part, min(M2, 2 * part + 2))
         quantise_w_in(0)
+        for part in HEAD2:
+            sort_x(0, x_sorted, 2 * part, min(M2, 2 * part + 2))
         for part in range(X_PARTS):
             turn_x(0, x_sorted, part)
             group_x(0, part, nc.scalar.copy)
@@ -393,6 +423,8 @@ def tile_feedforwardse3_pb_kernel(tc, x, w_in, scale, bias, w_out, out):
                     if drain:
                         root_of_unit(summed)
                         norm_mul(summed)
+                if m == 2 and step in GROUP_M2:
+                    group_w_out(GROUP_M2[step])
                 if step in TURN_X:
                     if 0 <= m - X_LATE < X_PARTS:
                         group_x(TURN_X[step], m - X_LATE, nc.vector.tensor_copy)
@@ -430,10 +462,13 @@ def tile_feedforwardse3_pb_kernel(tc, x, w_in, scale, bias, w_out, out):
             if step in TURN_X and X_LATE + X_PARTS > M2:
                 group_x(TURN_X[step], X_PARTS - 1, nc.vector.tensor_copy)
             if step in SORT_X:
-                x_sorted = sort_x(SORT_X[step])
+                x_sorted = new_sorted()
+                sort_x(SORT_X[step], x_sorted, 0, M2)
             if step == 1:
                 nc.vector.tensor_copy(out=gain[:], in_=gain_bf[:].rearrange("p g j -> p (g j)"))
                 nc.vector.tensor_copy(out=shift[:], in_=shift_bf[:].rearrange("p g j -> p (g j)"))
+            if step in GROUP_W:
+                group_w_out(GROUP_W[step])
             if step in W_OUT:
                 quantise_w_out(W_OUT[step])
         for m in range(M2):

from contextlib import ExitStack

import concourse.mybir as mybir
from concourse.masks import make_identity

F32 = mybir.dt.float32
BF16 = mybir.dt.bfloat16
U32 = mybir.dt.uint32
U8 = mybir.dt.uint8
FP8X4 = mybir.dt.float8_e4m3fn_x4
ACT = mybir.ActivationFunctionType
ALU = mybir.AluOpType

P = 128
PACK = 4
K_PASS = P * PACK
TOKEN_TILES = 4
D = 512
F = 2048
F_GROUPS = F // K_PASS
UNITS = TOKEN_TILES * F_GROUPS
RUN = 2
M2 = 5
EPS = 1e-12

SUM_PARTS = {1: (0, 4)}
CLAMP_M = 2
D_CLAMP = 1
D_SUM = 0
D_GELU = 3
OUT_M = (2, 4)
ROOT_LATE = 1
AHEAD = 1
HEAD1 = (0, 1, 2)
HEAD2 = ()
WG = 1
GROUP_M2 = {}
GROUP_W = {3: 0, 4: 1, 5: 2, 6: 3}
X_PARTS = 3
OUTS = (1, 1, 1, 2)
X_FIRST = 2
X_LATE = 3
SORT_X = {1: 1, 2: 2, 3: 3}
TURN_X = {2: 1, 3: 2, 4: 3}
W_OUT = {4: 0, 5: 1, 6: 2, 7: 3}
V_OUT = 1
V_COPIES = (2, 4)
STORE_S = 1
GELU_BATCH = 2
LEAD = GELU_BATCH + 2

FLOPS = 2 * 2 * (TOKEN_TILES * P * M2) * D * F


def tile_feedforwardse3_pb_kernel(tc, x, w_in, scale, bias, w_out, out):
    nc = tc.nc
    with ExitStack() as stack:
        consts = stack.enter_context(tc.tile_pool(name="consts", bufs=1))
        keep = stack.enter_context(tc.tile_pool(name="keep", bufs=1))
        x_rows_pool = stack.enter_context(tc.tile_pool(name="x_rows_pool", bufs=2))
        x_work = stack.enter_context(tc.tile_pool(name="x_work", bufs=1))
        w_rows_pool = stack.enter_context(tc.tile_pool(name="w_rows_pool", bufs=4))
        pairs_of = stack.enter_context(tc.tile_pool(name="pairs_of", bufs=2))
        two_batches = stack.enter_context(tc.tile_pool(name="two_batches", bufs=2 * GELU_BATCH))
        y_pool = stack.enter_context(tc.tile_pool(name="y_pool", bufs=2))
        psum_norm = stack.enter_context(tc.psum_pool(name="psum_norm", bufs=3))
        psum_gate = stack.enter_context(tc.psum_pool(name="psum_gate", bufs=3))
        psum_out = stack.enter_context(tc.psum_pool(name="psum_out", bufs=2))
        stack.enter_context(tc.manual_schedule())

        identity = consts.tile([P, P], F32)
        make_identity(nc, identity[:])

        x_codes = keep.tile([P, TOKEN_TILES, M2, P], U32, align_bytes=64)
        x_scales = keep.tile([P, TOKEN_TILES, M2, P], U8, align_bytes=64)
        w1_codes = keep.tile([P, F_GROUPS, K_PASS], U32, align_bytes=64)
        w1_scales = keep.tile([P, F_GROUPS, K_PASS], U8, align_bytes=64)
        w2_codes = keep.tile([P, F_GROUPS, D], U32, align_bytes=64)
        w2_scales = keep.tile([P, F_GROUPS, D], U8, align_bytes=64)

        def load_x(tt):
            x_rows = x_rows_pool.tile([P, D * M2], BF16, name="x_rows")
            nc.sync.dma_start(out=x_rows[:], in_=x[tt].rearrange("n d m -> n (d m)"))
            return x_rows

        def load_weight_rows(weight, fg, by_columns):
            w_rows = w_rows_pool.tile([P, PACK, K_PASS], BF16, name="w_rows")
            piece = slice(fg * K_PASS, (fg + 1) * K_PASS)
            source = weight[:, piece] if by_columns else weight[piece, :]
            nc.sync.dma_start(out=w_rows[:], in_=source.rearrange("(q s) c -> q s c", s=PACK))
            return w_rows

        x_rows_of = [load_x(0)]
        w_in_rows = [load_weight_rows(w_in, fg, True) for fg in range(F_GROUPS)]
        x_rows_of.append(load_x(1))
        w_out_rows = [load_weight_rows(w_out, fg, False) for fg in range(F_GROUPS)]
        x_rows_of.extend([load_x(2), load_x(3)])

        gain_bf = consts.tile([P, F_GROUPS, PACK], BF16)
        shift_bf = consts.tile([P, F_GROUPS, PACK], BF16)
        by_partition = "a b (g p j) -> p (a b g) j"
        nc.scalar.dma_start(out=gain_bf[:], in_=scale.rearrange(by_partition, p=P, j=PACK))
        nc.scalar.dma_start(out=shift_bf[:], in_=bias.rearrange(by_partition, p=P, j=PACK))
        gain = consts.tile([P, F_GROUPS * PACK], F32)
        shift = consts.tile([P, F_GROUPS * PACK], F32)

        def sort_x(tt, x_sorted, first, last):
            nc.vector.tensor_copy(
                out=x_sorted[:].rearrange("t (m u p e) -> t u m p e", m=M2, u=2, p=P, e=2)[
                    :, :, first:last, :, :
                ],
                in_=x_rows_of[tt][:].rearrange("t (p u e m) -> t u m p e", p=P, u=2, e=2, m=M2)[
                    :, :, first:last, :, :
                ],
            )

        def new_sorted():
            return x_work.tile([P, M2 * D], BF16, name="x_sorted")

        x_grouped_of = {}
        x_banks_of = {}

        def turn_x(tt, x_sorted, part):
            x_pairs = x_sorted[:].bitcast(F32)
            x_t = psum_out.tile([P, 2, 2, P], F32, tag="bank")
            x_banks_of[tt, part] = x_t
            for i in range(2 * min(2, M2 - 2 * part)):
                start = (4 * part + i) * P
                nc.tensor.transpose(
                    x_t[:, i // 2, i % 2, :], x_pairs[:, start : start + P], identity[:]
                )

        def group_x(tt, part, copy_out):
            if part == 0:
                x_grouped = x_work.tile([P, M2, K_PASS], BF16, name="x_grouped", align_bytes=64)
                x_grouped_of[tt] = x_grouped
            x_grouped = x_grouped_of[tt]
            first = 2 * part
            count = min(2, M2 - first)
            copy_out(
                out=x_grouped[:, first : first + count, :]
                .rearrange("p m k -> p (m k)")
                .bitcast(F32)
                .rearrange("p (m t u) -> p m t u", m=count, u=2),
                in_=x_banks_of[tt, part][:, 0:count, :, :].rearrange("p m u t -> p m t u"),
            )
            for m in range(first, first + count):
                nc.vector.quantize_mx(
                    out=x_codes[:, tt, m, :].bitcast(FP8X4),
                    scales=x_scales[:, tt, m, :],
                    in_=x_grouped[:, m, :],
                )

        def quantise_w_in(fg):
            w_grouped = pairs_of.tile([P, K_PASS * PACK], BF16, name="w_grouped", align_bytes=64)
            nc.vector.tensor_copy(
                out=w_grouped[:].rearrange("q (j p s) -> q j p s", j=PACK, p=P, s=PACK),
                in_=w_in_rows[fg][:].rearrange("q s (p j) -> q j p s", j=PACK),
            )
            nc.vector.quantize_mx(
                out=w1_codes[:, fg, :].bitcast(FP8X4), scales=w1_scales[:, fg, :], in_=w_grouped[:]
            )

        def quantise_w_out(fg):
            nc.vector.quantize_mx(
                out=w2_codes[:, fg, :].bitcast(FP8X4),
                scales=w2_scales[:, fg, :],
                in_=w_out_grouped[fg][:],
            )

        def group_w_out(fg):
            w_grouped = pairs_of.tile([P, D * PACK], BF16, name="w_grouped", align_bytes=64)
            w_out_grouped[fg] = w_grouped
            if WG:
                nc.gpsimd.tensor_scalar(
                    out=w_grouped[:].rearrange("p (d j) -> p d j", j=PACK),
                    in0=w_out_rows[fg][:].rearrange("p j d -> p d j"),
                    scalar1=1.0,
                    scalar2=0.0,
                    op0=ALU.mult,
                    op1=ALU.add,
                )
            else:
                nc.vector.tensor_copy(
                    out=w_grouped[:].rearrange("p (d j) -> p d j", j=PACK),
                    in_=w_out_rows[fg][:].rearrange("p j d -> p d j"),
                )

        w_out_grouped = {}
        squares_of = {}
        total_of = {}
        inv_norm_of = {}
        norm_of = {}
        gate_of = {}
        g_grouped_of = {}
        g_words_of = {}
        y_of = {}
        y_planes_of = {}

        def square_component(unit, m):
            tt, fg = divmod(unit, F_GROUPS)
            if m == 0:
                squares_of[unit] = pairs_of.tile([P, M2, K_PASS], F32, name="squares")
            h_rows = psum_norm.tile([P, K_PASS], F32)
            nc.tensor.matmul_mx(
                out=h_rows[:],
                lhsT=x_codes[:, tt, m, :].bitcast(FP8X4),
                lhsT_scale=x_scales[:, tt, m, :],
                rhs=w1_codes[:, fg, :].bitcast(FP8X4),
                rhs_scale=w1_scales[:, fg, :],
                start=True,
                stop=True,
            )
            nc.scalar.activation(out=squares_of[unit][:, m, :], in_=h_rows[:], func=ACT.Square)

        def sum_squares(unit, sums, first, last):
            for j in range(first, last):
                for m in range(M2):
                    nc.tensor.matmul(
                        out=sums[:, j, :],
                        lhsT=squares_of[unit][:, m, j * P : (j + 1) * P],
                        rhs=identity[:],
                        is_transpose=True,
                        start=(m == 0),
                        stop=(m == M2 - 1),
                    )

        def clamp_sums(unit, sums):
            total_of[unit] = two_batches.tile([P, K_PASS], F32, name="total")
            nc.vector.tensor_scalar_max(
                out=total_of[unit][:], in0=sums[:].rearrange("p j t -> p (j t)"), scalar1=EPS * EPS
            )

        def root_of_unit(unit):
            inv_norm_of[unit] = two_batches.tile([P, K_PASS], F32, name="inv_norm")
            nc.scalar.activation(
                out=inv_norm_of[unit][:], in_=total_of[unit][:], func=ACT.Abs_reciprocal_sqrt
            )

        def norm_mul(unit):
            norm_of[unit] = two_batches.tile([P, K_PASS], F32, name="norm")
            nc.gpsimd.tensor_tensor(
                out=norm_of[unit][:], in0=total_of[unit][:], in1=inv_norm_of[unit][:], op=ALU.mult
            )

        def gelu_of_unit(unit):
            fg = unit % F_GROUPS
            gelu = norm_of[unit]
            for j in range(PACK):
                cols = slice(j * P, (j + 1) * P)
                c = fg * PACK + j
                nc.scalar.activation(
                    out=gelu[:, cols],
                    in_=gelu[:, cols],
                    func=ACT.Gelu,
                    scale=gain[:, c : c + 1],
                    bias=shift[:, c : c + 1],
                )

        def gate_mul(unit):
            gelu = norm_of[unit]
            gate_of[unit] = two_batches.tile([P, P // RUN, PACK, RUN], F32, name="gate")
            nc.gpsimd.tensor_tensor(
                out=gate_of[unit][:],
                in0=gelu[:].rearrange("p (j q i) -> p q j i", j=PACK, i=RUN),
                in1=inv_norm_of[unit][:].rearrange("p (j q i) -> p q j i", j=PACK, i=RUN),
                op=ALU.mult,
            )

        def gate_component(unit, m):
            tt, fg = divmod(unit, F_GROUPS)
            if m == 0:
                g_grouped_of[unit] = pairs_of.tile(
                    [P, M2, P, PACK], BF16, name="g_grouped", align_bytes=64
                )
            h = psum_gate.tile([P, PACK, P], F32)
            for j in range(PACK):
                cols = slice(j * P, (j + 1) * P)
                nc.tensor.matmul_mx(
                    out=h[:, j, :],
                    lhsT=w1_codes[:, fg, cols].bitcast(FP8X4),
                    lhsT_scale=w1_scales[:, fg, cols],
                    rhs=x_codes[:, tt, m, :].bitcast(FP8X4),
                    rhs_scale=x_scales[:, tt, m, :],
                    start=True,
                    stop=True,
                )
            nc.vector.tensor_tensor(
                out=g_grouped_of[unit][:, m, :, :].rearrange("p (q i) j -> p q j i", i=RUN),
                in0=h[:].rearrange("p j (q i) -> p q j i", i=RUN),
                in1=gate_of[unit][:],
                op=ALU.mult,
            )

        def quantise_g(unit, pieces=((0, 4), (4, 5))):
            tt, fg = divmod(unit, F_GROUPS)
            if fg == 0:
                g_words_of[tt] = (
                    pairs_of.tile([P, F_GROUPS, M2, P], U32, name="g_codes", align_bytes=64),
                    pairs_of.tile([P, F_GROUPS, M2, P], U8, name="g_scales", align_bytes=64),
                )
            g_codes, g_scales = g_words_of[tt]
            for first, last in pieces:
                nc.vector.quantize_mx(
                    out=g_codes[:, fg, first:last, :].rearrange("p m t -> p (m t)").bitcast(FP8X4),
                    scales=g_scales[:, fg, first:last, :].rearrange("p m t -> p (m t)"),
                    in_=g_grouped_of[unit][:, first:last, :, :].rearrange("p m t j -> p (m t j)"),
                )

        def output_passes(tt, m, first, last):
            if first == 0:
                if m == 0:
                    y_planes_of[tt] = y_pool.tile([P, M2, D], F32, name="y_planes")
                if tt == TOKEN_TILES - 1 and m < 3:
                    h_rows = psum_norm.tile([P, D], F32)
                    y_of[tt, m] = h_rows
                else:
                    y = psum_out.tile([P, D], F32, tag="bank")
                    y_of[tt, m] = y
            g_codes, g_scales = g_words_of[tt]
            for fg in range(first, last):
                nc.tensor.matmul_mx(
                    out=y_of[tt, m][:],
                    lhsT=g_codes[:, fg, m, :].bitcast(FP8X4),
                    lhsT_scale=g_scales[:, fg, m, :],
                    rhs=w2_codes[:, fg, :].bitcast(FP8X4),
                    rhs_scale=w2_scales[:, fg, :],
                    start=(fg == 0),
                    stop=(fg == F_GROUPS - 1),
                )

        def output_copy(tt, m, copy):
            copy(out=y_planes_of[tt][:, m, :], in_=y_of[tt, m][:])

        def store_tile(tt):
            half = D // 2
            planes = y_planes_of[tt][:].rearrange("t m d -> t d m")
            rows = out[tt].rearrange("n d m -> n (d m)")
            if tt == TOKEN_TILES - 2 and STORE_S:
                copy_low = copy_high = nc.scalar.copy
            elif tt == TOKEN_TILES - 1:
                copy_low = copy_high = nc.vector.tensor_copy
            else:
                copy_low = nc.vector.tensor_copy
                copy_high = None
            y_low = pairs_of.tile([P, half, M2], F32, name="y_low")
            copy_low(out=y_low[:], in_=planes[:, 0:half, :])
            nc.sync.dma_start(
                out=rows[:, 0 : half * M2], in_=y_low[:].rearrange("t d m -> t (d m)")
            )
            y_high = pairs_of.tile([P, half, M2], F32, name="y_high")
            if copy_high:
                copy_high(out=y_high[:], in_=planes[:, half:D, :])
            else:
                nc.gpsimd.tensor_scalar(
                    out=y_high[:],
                    in0=planes[:, half:D, :],
                    scalar1=1.0,
                    scalar2=0.0,
                    op0=ALU.mult,
                    op1=ALU.add,
                )
            nc.sync.dma_start(
                out=rows[:, half * M2 : D * M2], in_=y_high[:].rearrange("t d m -> t (d m)")
            )

        x_sorted = new_sorted()
        for part in HEAD1:
            sort_x(0, x_sorted, 2 * part, min(M2, 2 * part + 2))
        quantise_w_in(0)
        for part in HEAD2:
            sort_x(0, x_sorted, 2 * part, min(M2, 2 * part + 2))
        for part in range(X_PARTS):
            turn_x(0, x_sorted, part)
            group_x(0, part, nc.scalar.copy)
        for fg in range(1, F_GROUPS):
            quantise_w_in(fg)

        last = TOKEN_TILES - 1
        outs = []
        written = None
        for step in range(UNITS + LEAD):
            squared = step
            summed = step - 1
            rooted = step - 2
            gated = step - LEAD
            drain = step == UNITS

            gelu_step = 0 <= rooted < UNITS - 1 and rooted % GELU_BATCH == GELU_BATCH - 1
            batch_start = rooted - (GELU_BATCH - 1)
            for m in range(M2):
                if squared < UNITS and not (step == 0 and m == 0):
                    for beat in range(M2 * step + m + AHEAD, M2 * step + m + AHEAD + 1):
                        if beat < M2 * UNITS:
                            square_component(*divmod(beat, M2))
                if step == 0 and m == 0:
                    for beat in range(AHEAD + 1):
                        square_component(0, beat)
                if 0 <= rooted < UNITS - 1 and m == 0:
                    norm_mul(rooted)
                if gelu_step and m < GELU_BATCH:
                    gelu_of_unit(batch_start + m)
                if gelu_step and 1 <= m <= GELU_BATCH:
                    gate_mul(batch_start + m - 1)
                if drain and m == D_GELU:
                    for unit in range(UNITS - GELU_BATCH, UNITS):
                        gelu_of_unit(unit)
                        gate_mul(unit)
                if 0 <= gated < UNITS:
                    gate_component(gated, m)
                if gated == UNITS - 1 and m:
                    quantise_g(gated, ((m - 1, m),))
                if drain and m == D_SUM:
                    h_rows = psum_norm.tile([P, PACK, P], F32)
                    sums = h_rows
                    sum_squares(summed, sums, 0, PACK)
                if 0 <= summed < UNITS and m in SUM_PARTS and not drain:
                    if SUM_PARTS[m][0] == 0:
                        sums = psum_out.tile([P, PACK, P], F32, tag="bank")
                    sum_squares(summed, sums, *SUM_PARTS[m])
                if 0 <= summed < UNITS and m == (D_CLAMP if drain else CLAMP_M):
                    clamp_sums(summed, sums)
                    if drain:
                        root_of_unit(summed)
                        norm_mul(summed)
                if m == 2 and step in GROUP_M2:
                    group_w_out(GROUP_M2[step])
                if step in TURN_X:
                    if 0 <= m - X_LATE < X_PARTS:
                        group_x(TURN_X[step], m - X_LATE, nc.vector.tensor_copy)
                    if 0 <= m - X_FIRST < X_PARTS:
                        turn_x(TURN_X[step], x_sorted, m - X_FIRST)
                if step >= UNITS and outs and m in OUT_M:
                    output_passes(*outs[0], 0, F_GROUPS)
                    output_copy(*outs.pop(0), nc.scalar.copy)
                    if not outs:
                        store_tile(last - 1)
                if gated == UNITS - 2:
                    output_passes(last, m, 0, F_GROUPS - 2)
                if gated == UNITS - 1:
                    output_passes(last, m, F_GROUPS - 2, F_GROUPS - 1)
            if 0 <= gated < UNITS - 1:
                quantise_g(gated)
                if written is not None:
                    store_tile(written)
                    written = None
            elif gated == UNITS - 1:
                quantise_g(gated, ((M2 - 1, M2),))
            if 0 <= summed < UNITS and not drain and not ROOT_LATE:
                root_of_unit(summed)
            if step < UNITS and outs:
                for i in range(OUTS[step % F_GROUPS]):
                    if outs:
                        output_passes(*outs[0], 0, F_GROUPS)
                        output_copy(*outs.pop(0), nc.vector.tensor_copy if V_OUT else nc.scalar.copy)
                if not outs:
                    written = gated // F_GROUPS - 1
            if 0 <= summed < UNITS and not drain and ROOT_LATE:
                root_of_unit(summed)
            if 0 <= gated < UNITS - F_GROUPS and gated % F_GROUPS == F_GROUPS - 1:
                outs = [(gated // F_GROUPS, m) for m in range(M2)]
            if step in TURN_X and X_LATE + X_PARTS > M2:
                group_x(TURN_X[step], X_PARTS - 1, nc.vector.tensor_copy)
            if step in SORT_X:
                x_sorted = new_sorted()
                sort_x(SORT_X[step], x_sorted, 0, M2)
            if step == 1:
                nc.vector.tensor_copy(out=gain[:], in_=gain_bf[:].rearrange("p g j -> p (g j)"))
                nc.vector.tensor_copy(out=shift[:], in_=shift_bf[:].rearrange("p g j -> p (g j)"))
            if step in GROUP_W:
                group_w_out(GROUP_W[step])
            if step in W_OUT:
                quantise_w_out(W_OUT[step])
        for m in range(M2):
            output_passes(last, m, F_GROUPS - 1, F_GROUPS)
            output_copy(last, m, nc.vector.tensor_copy if m in V_COPIES else nc.scalar.copy)
        store_tile(last)
